import numpy as np
import ml_dtypes


def mxq(x, axis, fmt="e4m3"):
    dtype, down = {"e4m3": (ml_dtypes.float8_e4m3fn, 7), "e5m2": (ml_dtypes.float8_e5m2, 14)}[fmt]
    v = np.moveaxis(np.asarray(x, np.float32).astype(ml_dtypes.bfloat16).astype(np.float64), axis, -1)
    blocks = v.reshape(v.shape[:-1] + (-1, 32))
    amax = np.abs(blocks).max(-1, keepdims=True)
    byte = np.maximum(np.where(amax > 0, np.frexp(amax)[1] - 1 + 127, 0) - down, 1)
    scale = np.exp2(byte - 127.0)
    codes = (blocks / scale).astype(np.float32).astype(dtype).astype(np.float64)
    return np.moveaxis((codes * scale).reshape(v.shape), -1, axis)


WIDE = False


def mx_kscale(k):
    if not WIDE:
        return np.ones(k)
    levels = np.array([10, -10, 5, -5, 0])
    if k % 512:
        return np.exp2(np.random.permutation(np.resize(levels, k // 32))).repeat(32)
    a = np.empty((k // 512, 16))
    for p in range(k // 512):
        a[p, :8] = np.random.permutation(np.resize(levels, 8))
        for g in range(8):
            far = levels[np.abs(levels - a[p, g]) >= 10]
            a[p, g + 8] = far[np.random.randint(len(far))]
    return np.exp2(a.ravel()).repeat(32)


BF16 = ml_dtypes.bfloat16


def bf(x):
    return np.asarray(x, np.float32).astype(BF16)


def f64(x):
    return np.asarray(x).astype(np.float64)


NK, F, B = 12288, 512, 256
D = 2 * F
EPS = 1e-8


def rotate_half(x):
    d = x.shape[-1] // 2
    return np.concatenate([-x[..., d:], x[..., :d]], axis=-1)


def setup_inputs():
    sf = mx_kscale(F)
    s = np.concatenate([sf, sf])
    c = np.exp2(np.round(0.5 * np.log2(np.mean(1.0 / s**2))))
    return {"K": bf(np.random.standard_normal((NK, D)) * s * c),
            "reference_angles": bf(np.random.random(F) * 2.0 * np.pi),
            "probes": bf(np.random.standard_normal((B, D)) / s),
            "u_weights": bf(np.random.standard_normal((B, F)) * 0.5 / np.sqrt(F) / (sf * c)),
            "k_bias": bf(np.random.standard_normal(B) * 0.5)}


def reference(K, reference_angles, probes, u_weights, k_bias):
    K = f64(K)
    probes = f64(probes)
    pnorm = np.sqrt(np.sum(probes**2, axis=-1, keepdims=True))
    p = probes / (pnorm + EPS)
    theta_full = np.concatenate([f64(reference_angles), f64(reference_angles)], axis=-1)
    rotated = p * np.cos(theta_full) + rotate_half(p) * np.sin(theta_full)
    dot_term = mxq(K, 1, "e4m3") @ mxq(rotated, 1, "e4m3").T
    K_mag = np.sqrt(K[..., :F] ** 2 + K[..., F:] ** 2 + EPS)
    logits = dot_term + (mxq(K_mag, 1, "e4m3") @ mxq(f64(u_weights), 1, "e4m3").T) + f64(k_bias)
    return logits

@@ -1,0 +1,337 @@
+from contextlib import ExitStack
+
+import concourse.mybir as mybir
+from concourse.masks import make_identity
+
+F32 = mybir.dt.float32
+BF16 = mybir.dt.bfloat16
+U32 = mybir.dt.uint32
+U8 = mybir.dt.uint8
+FP8X4 = mybir.dt.float8_e4m3fn_x4
+ACT = mybir.ActivationFunctionType
+ALU = mybir.AluOpType
+
+N_KEYS, D, F, B = 12288, 1024, 512, 256
+EPS = 1e-8
+FLOPS = 2 * N_KEYS * B * (D + F)
+
+P = 128
+PACK = 4
+TILES = 2
+N_PAIRS = N_KEYS // (TILES * P)
+KEY_BUFS = 6
+VECTOR_SQUARES = TILES * D // 8
+MX_LAG = 5
+
+TWO_PI_HI = 6.28125
+TWO_PI_MID = 0.0019353071693331003189
+TWO_PI_LO = 1.0253131677018245682e-11
+INV_TWO_PI = 0.15915493667125701904
+ROUND_MAGIC = 12582912.0
+PI_BELOW = 3.1415925025939941406
+
+
+def tile_module2network_t_kernel(tc, K, reference_angles, probes, u_weights, k_bias, out):
+    nc = tc.nc
+    with ExitStack() as ctx:
+        const = ctx.enter_context(tc.tile_pool(name="const", bufs=1))
+        setup = ctx.enter_context(tc.tile_pool(name="setup", bufs=1))
+        setup_tmp = ctx.enter_context(tc.tile_pool(name="setup_tmp", bufs=2))
+        key_pool = ctx.enter_context(tc.tile_pool(name="keys", bufs=KEY_BUFS))
+        square_pool = ctx.enter_context(tc.tile_pool(name="squares", bufs=3))
+        grouped_pool = ctx.enter_context(tc.tile_pool(name="grouped", bufs=3))
+        key_code_pool = ctx.enter_context(tc.tile_pool(name="key_codes", bufs=MX_LAG + 3))
+        mag_pool = ctx.enter_context(tc.tile_pool(name="mag", bufs=4))
+        mag_code_pool = ctx.enter_context(tc.tile_pool(name="mag_codes", bufs=6))
+        logit_pool = ctx.enter_context(tc.tile_pool(name="logits", bufs=4))
+        keyT_psum = ctx.enter_context(tc.psum_pool(name="keyT_psum", bufs=2))
+        sum_psum = ctx.enter_context(tc.psum_pool(name="sum_psum", bufs=4))
+        acc_psum = ctx.enter_context(tc.psum_pool(name="acc_psum", bufs=2))
+
+        K_pairs = K.rearrange("(j p t) d -> j p (t d)", p=P, t=TILES)
+        out_pairs = out.rearrange("(j p t) b -> j p (t b)", p=P, t=TILES)
+
+        angles = setup.tile([P, PACK], BF16)
+        nc.scalar.dma_start(out=angles[:], in_=reference_angles.rearrange("(p k) -> p k", k=PACK))
+        probes_sb = setup.tile([P, 2, D], BF16)
+        nc.scalar.dma_start(out=probes_sb[:], in_=probes.rearrange("(h p) d -> p h d", p=P))
+        u_sb = setup.tile([P, 2, F], BF16)
+        nc.scalar.dma_start(out=u_sb[:], in_=u_weights.rearrange("(h p) f -> p h f", p=P))
+        bias_rows = const.tile([P, B], BF16)
+        nc.scalar.dma_start(out=bias_rows[:], in_=k_bias.partition_broadcast(P))
+
+        ident_f32 = const.tile([P, P], F32)
+        make_identity(nc, ident_f32[:])
+        ident_bf16 = const.tile([P, P], BF16)
+        make_identity(nc, ident_bf16[:])
+        eps_col = const.tile([P, 1], F32)
+        nc.vector.memset(eps_col[:], EPS)
+
+        keys, keysT, squares, grouped = {}, {}, {}, {}
+        key_codes, sums, mags, mag_codes, accs = {}, {}, {}, {}, {}
+
+        def load_keys(j):
+            k_sb = key_pool.tile([P, TILES, D], BF16)
+            nc.sync.dma_start(out=k_sb[:].rearrange("p t d -> p (t d)"), in_=K_pairs[j])
+            keys[j] = k_sb
+
+        def transpose_keys(j, t):
+            words = keys[j][:].bitcast(F32)
+            kT = keyT_psum.tile([P, PACK, P], F32)
+            for g in range(2):
+                for u in range(2):
+                    nc.tensor.transpose(
+                        kT[:, 2 * g + u, :],
+                        words[:, t, 2 * g * P + u : 2 * (g + 1) * P : 2],
+                        ident_f32[:],
+                    )
+            keysT[(j, t)] = kT
+
+        def regroup_keys(j):
+            kg = grouped_pool.tile([P, 2, TILES, P, PACK], BF16, align_bytes=64)
+            kg_words = kg[:].bitcast(F32)
+            for t in range(TILES):
+                nc.vector.tensor_copy(
+                    out=kg_words[:, :, t, :, :],
+                    in_=keysT[(j, t)][:].rearrange("p (g u) n -> p g n u", u=2),
+                )
+            grouped[j] = kg
+
+        def quantise_keys(j):
+            kc = key_code_pool.tile([P, 2 * TILES * P], U32, align_bytes=64)
+            ks = key_code_pool.tile([P, 2 * TILES * P], U8, align_bytes=64)
+            nc.vector.quantize_mx(
+                out=kc[:].bitcast(FP8X4),
+                scales=ks[:],
+                in_=grouped[j][:].rearrange("p g t n k -> p (g t n k)"),
+            )
+            key_codes[j] = (kc, ks)
+
+        def square_keys(j):
+            sq = square_pool.tile([P, TILES, D], F32)
+            sq_kp = sq[:].rearrange("p t (g k f) -> p (t g) k f", g=2, k=PACK)
+            k_kp = keys[j][:].rearrange("p t (g f k) -> p (t g) k f", g=2, k=PACK)
+            last = 2 * TILES - 1
+            nc.scalar.activation(out=sq_kp[:, 0:last], in_=k_kp[:, 0:last], func=ACT.Square)
+            cut = PACK - VECTOR_SQUARES // P
+            nc.scalar.activation(out=sq_kp[:, last, 0:cut], in_=k_kp[:, last, 0:cut], func=ACT.Square)
+            nc.vector.tensor_tensor(
+                out=sq_kp[:, last, cut:], in0=k_kp[:, last, cut:], in1=k_kp[:, last, cut:], op=ALU.mult
+            )
+            squares[j] = sq
+
+        def add_odd_tiles(j):
+            for t in range(1, TILES, 2):
+                nc.gpsimd.tensor_tensor(
+                    out=squares[j][:, t, 0:F],
+                    in0=squares[j][:, t, 0:F],
+                    in1=squares[j][:, t, F:D],
+                    op=ALU.add,
+                )
+
+        def transpose_sums(j, t):
+            terms = 2 if t % 2 == 0 else 1
+            s_ps = sum_psum.tile([P, PACK, P], F32)
+            for k in range(PACK):
+                for g in range(terms):
+                    nc.tensor.matmul(
+                        out=s_ps[:, k, :],
+                        lhsT=squares[j][:, t, g * F + k * P : g * F + (k + 1) * P],
+                        rhs=ident_f32[:],
+                        is_transpose=True,
+                        start=(g == 0),
+                        stop=(g == terms - 1),
+                    )
+            sums[(j, t)] = s_ps
+
+        def root_magnitudes(j):
+            mg = mag_pool.tile([P, TILES, P, PACK], BF16, align_bytes=64)
+            for t in range(TILES):
+                nc.scalar.activation(
+                    out=mg[:, t, :, :],
+                    in_=sums[(j, t)][:].rearrange("p k n -> p n k"),
+                    func=ACT.Sqrt,
+                    bias=eps_col[:, 0:1],
+                )
+            mags[j] = mg
+
+        def quantise_magnitudes(j):
+            mc = mag_code_pool.tile([P, TILES * P], U32, align_bytes=64)
+            ms = mag_code_pool.tile([P, TILES * P], U8, align_bytes=64)
+            nc.vector.quantize_mx(
+                out=mc[:].bitcast(FP8X4),
+                scales=ms[:],
+                in_=mags[j][:].rearrange("p t n k -> p (t n k)"),
+            )
+            mag_codes[j] = (mc, ms)
+
+        def multiply(j, t):
+            kc, ks = key_codes[j]
+            mc, ms = mag_codes[j]
+            if t == 0:
+                acc = acc_psum.tile([P, TILES, B], F32)
+                accs[j] = acc
+            for g in range(2):
+                key_cols = slice((g * TILES + t) * P, (g * TILES + t + 1) * P)
+                nc.tensor.matmul_mx(
+                    out=accs[j][:, t, :],
+                    lhsT=kc[:, key_cols].bitcast(FP8X4),
+                    lhsT_scale=ks[:, key_cols],
+                    rhs=rot_codes[:, g * B : (g + 1) * B].bitcast(FP8X4),
+                    rhs_scale=rot_scales[:, g * B : (g + 1) * B],
+                    start=(g == 0),
+                    stop=False,
+                )
+            nc.tensor.matmul_mx(
+                out=accs[j][:, t, :],
+                lhsT=mc[:, t * P : (t + 1) * P].bitcast(FP8X4),
+                lhsT_scale=ms[:, t * P : (t + 1) * P],
+                rhs=u_codes[:].bitcast(FP8X4),
+                rhs_scale=u_scales[:],
+                start=False,
+                stop=True,
+            )
+
+        def add_bias_and_store(j):
+            logits = logit_pool.tile([P, TILES, B], F32)
+            nc.vector.tensor_tensor(
+                out=logits[:],
+                in0=accs[j][:],
+                in1=bias_rows[:].unsqueeze(1).to_broadcast([P, TILES, B]),
+                op=ALU.add,
+            )
+            nc.sync.dma_start(out=out_pairs[j], in_=logits[:].rearrange("p t b -> p (t b)"))
+
+        def run(stage, j, *tile_index):
+            if 0 <= j < N_PAIRS:
+                stage(j, *tile_index)
+
+        for j in range(KEY_BUFS):
+            load_keys(j)
+
+        uT = acc_psum.tile([P, PACK, B], BF16, tag="acc")
+        for h in range(2):
+            for k in range(PACK):
+                nc.tensor.transpose(
+                    uT[:, k, h * P : (h + 1) * P], u_sb[:, h, k::PACK], ident_bf16[:]
+                )
+        u_grouped = setup.tile([P, B, PACK], BF16, align_bytes=64)
+        nc.vector.tensor_copy(out=u_grouped[:], in_=uT[:].rearrange("p k b -> p b k"))
+        u_codes = const.tile([P, B], U32, align_bytes=64)
+        u_scales = const.tile([P, B], U8, align_bytes=64)
+        nc.vector.quantize_mx(
+            out=u_codes[:].bitcast(FP8X4),
+            scales=u_scales[:],
+            in_=u_grouped[:].rearrange("p b k -> p (b k)"),
+        )
+
+        shift = setup.tile([P, 2, PACK], F32)
+        nc.vector.memset(shift[:, 0, :], 0.0)
+        nc.vector.memset(shift[:, 1, :], 0.25)
+        theta = setup.tile([P, 2, PACK], F32)
+        nc.vector.tensor_copy(out=theta[:], in_=angles[:].unsqueeze(1).to_broadcast([P, 2, PACK]))
+        turns = setup.tile([P, 2, PACK], F32)
+        nc.vector.scalar_tensor_tensor(
+            out=turns[:], in0=theta[:], scalar=INV_TWO_PI, in1=shift[:], op0=ALU.mult, op1=ALU.add
+        )
+        whole = setup.tile([P, 2, PACK], F32)
+        nc.vector.tensor_scalar_add(out=whole[:], in0=turns[:], scalar1=ROUND_MAGIC)
+        q = setup.tile([P, 2, PACK], F32)
+        nc.vector.scalar_tensor_tensor(
+            out=q[:], in0=whole[:], scalar=ROUND_MAGIC, in1=shift[:], op0=ALU.subtract, op1=ALU.subtract
+        )
+        reduced_a = setup.tile([P, 2, PACK], F32)
+        nc.vector.scalar_tensor_tensor(
+            out=reduced_a[:], in0=q[:], scalar=-TWO_PI_HI, in1=theta[:], op0=ALU.mult, op1=ALU.add
+        )
+        reduced_b = setup.tile([P, 2, PACK], F32)
+        nc.vector.scalar_tensor_tensor(
+            out=reduced_b[:], in0=q[:], scalar=-TWO_PI_MID, in1=reduced_a[:], op0=ALU.mult, op1=ALU.add
+        )
+        reduced_c = setup.tile([P, 2, PACK], F32)
+        nc.vector.scalar_tensor_tensor(
+            out=reduced_c[:], in0=q[:], scalar=-TWO_PI_LO, in1=reduced_b[:], op0=ALU.mult, op1=ALU.add
+        )
+        reduced = setup.tile([P, 2, PACK], F32)
+        nc.vector.tensor_scalar(
+            out=reduced[:], in0=reduced_c[:], scalar1=PI_BELOW, scalar2=-PI_BELOW, op0=ALU.min, op1=ALU.max
+        )
+        sin_cos = setup.tile([P, 2, PACK], F32)
+        nc.scalar.activation(out=sin_cos[:], in_=reduced[:], func=ACT.Sin)
+
+        squared_probes = setup.tile([P, 2, D], BF16)
+        norm_sq = setup.tile([P, 2], F32)
+        for h in range(2):
+            nc.scalar.activation(
+                out=squared_probes[:, h, :],
+                in_=probes_sb[:, h, :],
+                func=ACT.Square,
+                accum_out=norm_sq[:, h : h + 1],
+            )
+        norm = setup.tile([P, 2], F32)
+        nc.scalar.activation(out=norm[:], in_=norm_sq[:], func=ACT.Sqrt)
+        norm_eps = setup.tile([P, 2], F32)
+        nc.vector.tensor_scalar_add(out=norm_eps[:], in0=norm[:], scalar1=EPS)
+        inv_norm = setup.tile([P, 2], F32)
+        nc.vector.reciprocal(out=inv_norm[:], in_=norm_eps[:])
+        unit = setup.tile([P, 2, D], F32)
+        for h in range(2):
+            nc.vector.tensor_scalar_mul(
+                out=unit[:, h, :], in0=probes_sb[:, h, :], scalar1=inv_norm[:, h : h + 1]
+            )
+        unit_blocks = unit[:].rearrange("b h (g p k) -> b h g k p", g=2, k=PACK)
+        planes = setup.tile([P, 2, PACK, B], BF16)
+        for u in range(2):
+            re_ps = acc_psum.tile([P, 2, B], F32, tag="acc")
+            im_ps = acc_psum.tile([P, 2, B], F32, tag="acc")
+            for e in range(2):
+                for h in range(2):
+                    nc.tensor.transpose(
+                        re_ps[:, e, h * P : (h + 1) * P], unit_blocks[:, h, 0, 2 * u + e, :], ident_f32[:]
+                    )
+                    nc.tensor.transpose(
+                        im_ps[:, e, h * P : (h + 1) * P], unit_blocks[:, h, 1, 2 * u + e, :], ident_f32[:]
+                    )
+            for e in range(2):
+                c = 2 * u + e
+                sin_col = sin_cos[:, 0, c : c + 1]
+                cos_col = sin_cos[:, 1, c : c + 1]
+                im_sin = setup_tmp.tile([P, B], F32)
+                nc.vector.tensor_scalar_mul(out=im_sin[:], in0=im_ps[:, e, :], scalar1=sin_col)
+                nc.vector.scalar_tensor_tensor(
+                    out=planes[:, 0, c, :], in0=re_ps[:, e, :], scalar=cos_col, in1=im_sin[:],
+                    op0=ALU.mult, op1=ALU.subtract,
+                )
+                re_sin = setup_tmp.tile([P, B], F32)
+                nc.vector.tensor_scalar_mul(out=re_sin[:], in0=re_ps[:, e, :], scalar1=sin_col)
+                nc.vector.scalar_tensor_tensor(
+                    out=planes[:, 1, c, :], in0=im_ps[:, e, :], scalar=cos_col, in1=re_sin[:],
+                    op0=ALU.mult, op1=ALU.add,
+                )
+        rot_grouped = setup.tile([P, 2, B, PACK], BF16, align_bytes=64)
+        nc.vector.tensor_copy(out=rot_grouped[:], in_=planes[:].rearrange("p g k b -> p g b k"))
+        rot_codes = const.tile([P, 2 * B], U32, align_bytes=64)
+        rot_scales = const.tile([P, 2 * B], U8, align_bytes=64)
+        nc.vector.quantize_mx(
+            out=rot_codes[:].bitcast(FP8X4),
+            scales=rot_scales[:],
+            in_=rot_grouped[:].rearrange("p g b k -> p (g b k)"),
+        )
+
+        with tc.manual_schedule():
+            for t in range(TILES):
+                transpose_keys(0, t)
+            square_keys(0)
+            for step in range(N_PAIRS + MX_LAG + 1):
+                run(add_odd_tiles, step)
+                run(regroup_keys, step)
+                run(square_keys, step + 1)
+                run(load_keys, step + KEY_BUFS)
+                run(quantise_magnitudes, step - 2)
+                for t in range(TILES):
+                    run(transpose_keys, step + 1, t)
+                    run(transpose_sums, step, t)
+                    run(multiply, step - MX_LAG, t)
+                run(quantise_keys, step)
+                run(root_magnitudes, step - 1)
+                run(add_bias_and_store, step - MX_LAG - 1)

@@ -20,8 +20,10 @@ PACK = 4
 TILES = 2
 N_PAIRS = N_KEYS // (TILES * P)
 KEY_BUFS = 6
-VECTOR_SQUARES = TILES * D // 8
+GPSIMD_BLOCKS = 2
+VECTOR_FROM = 112
 MX_LAG = 5
+OUT_LAG = MX_LAG + 1
 
 TWO_PI_HI = 6.28125
 TWO_PI_MID = 0.0019353071693331003189
@@ -38,14 +40,15 @@ def tile_module2network_t_kernel(tc, K, reference_angles, probes, u_weights, k_b
         setup = ctx.enter_context(tc.tile_pool(name="setup", bufs=1))
         setup_tmp = ctx.enter_context(tc.tile_pool(name="setup_tmp", bufs=2))
         key_pool = ctx.enter_context(tc.tile_pool(name="keys", bufs=KEY_BUFS))
-        square_pool = ctx.enter_context(tc.tile_pool(name="squares", bufs=3))
-        grouped_pool = ctx.enter_context(tc.tile_pool(name="grouped", bufs=3))
+        nsquare_pool = ctx.enter_context(tc.tile_pool(name="natural_squares", bufs=3))
+        gsquare_pool = ctx.enter_context(tc.tile_pool(name="grouped_squares", bufs=4))
+        grouped_pool = ctx.enter_context(tc.tile_pool(name="grouped", bufs=4))
         key_code_pool = ctx.enter_context(tc.tile_pool(name="key_codes", bufs=MX_LAG + 3))
         mag_pool = ctx.enter_context(tc.tile_pool(name="mag", bufs=4))
         mag_code_pool = ctx.enter_context(tc.tile_pool(name="mag_codes", bufs=6))
         logit_pool = ctx.enter_context(tc.tile_pool(name="logits", bufs=4))
-        keyT_psum = ctx.enter_context(tc.psum_pool(name="keyT_psum", bufs=2))
-        sum_psum = ctx.enter_context(tc.psum_pool(name="sum_psum", bufs=4))
+        keyT_psum = ctx.enter_context(tc.psum_pool(name="keyT_psum", bufs=4))
+        sum_psum = ctx.enter_context(tc.psum_pool(name="sum_psum", bufs=2))
         acc_psum = ctx.enter_context(tc.psum_pool(name="acc_psum", bufs=2))
 
         K_pairs = K.rearrange("(j p t) d -> j p (t d)", p=P, t=TILES)
@@ -67,7 +70,7 @@ def tile_module2network_t_kernel(tc, K, reference_angles, probes, u_weights, k_b
         eps_col = const.tile([P, 1], F32)
         nc.vector.memset(eps_col[:], EPS)
 
-        keys, keysT, squares, grouped = {}, {}, {}, {}
+        keys, keysT, natural_squares, grouped, grouped_squares = {}, {}, {}, {}, {}
         key_codes, sums, mags, mag_codes, accs = {}, {}, {}, {}, {}
 
         def load_keys(j):
@@ -107,52 +110,68 @@ def tile_module2network_t_kernel(tc, K, reference_angles, probes, u_weights, k_b
             )
             key_codes[j] = (kc, ks)
 
-        def square_keys(j):
-            sq = square_pool.tile([P, TILES, D], F32)
-            sq_kp = sq[:].rearrange("p t (g k f) -> p (t g) k f", g=2, k=PACK)
-            k_kp = keys[j][:].rearrange("p t (g f k) -> p (t g) k f", g=2, k=PACK)
-            last = 2 * TILES - 1
-            nc.scalar.activation(out=sq_kp[:, 0:last], in_=k_kp[:, 0:last], func=ACT.Square)
-            cut = PACK - VECTOR_SQUARES // P
-            nc.scalar.activation(out=sq_kp[:, last, 0:cut], in_=k_kp[:, last, 0:cut], func=ACT.Square)
-            nc.vector.tensor_tensor(
-                out=sq_kp[:, last, cut:], in0=k_kp[:, last, cut:], in1=k_kp[:, last, cut:], op=ALU.mult
-            )
-            squares[j] = sq
-
-        def add_odd_tiles(j):
-            for t in range(1, TILES, 2):
-                nc.gpsimd.tensor_tensor(
-                    out=squares[j][:, t, 0:F],
-                    in0=squares[j][:, t, 0:F],
-                    in1=squares[j][:, t, F:D],
-                    op=ALU.add,
+        def square_last_keys(j):
+            sq = gsquare_pool.tile([P, 2, P, PACK], F32)
+            transposed = keysT[(j, 0)][:].bitcast(BF16).rearrange("p (g u) (n e) -> p g n u e", u=2, e=2)
+            for g in range(2):
+                nc.vector.tensor_tensor(
+                    out=sq[:, g, VECTOR_FROM:, :].rearrange("p n (u e) -> p n u e", u=2),
+                    in0=transposed[:, g, VECTOR_FROM:],
+                    in1=grouped[j][:, g, 0, VECTOR_FROM:, :].rearrange("p n (u e) -> p n u e", u=2),
+                    op=ALU.mult,
                 )
+            grouped_squares[j] = sq
 
-        def transpose_sums(j, t):
-            terms = 2 if t % 2 == 0 else 1
+        def square_grouped(j):
+            nc.scalar.activation(
+                out=grouped_squares[j][:, :, 0:VECTOR_FROM, :].rearrange("p g n k -> p g (n k)"),
+                in_=grouped[j][:, :, 0, 0:VECTOR_FROM, :].rearrange("p g n k -> p g (n k)"),
+                func=ACT.Square,
+            )
+
+        def add_grouped(j):
+            sq = grouped_squares[j]
+            nc.gpsimd.tensor_tensor(out=sq[:, 0], in0=sq[:, 0], in1=sq[:, 1], op=ALU.add)
+
+        def square_natural(j):
+            sq = nsquare_pool.tile([P, 2, PACK, P], F32)
+            k_kp = keys[j][:, 1, :].rearrange("p (g f k) -> p g k f", g=2, k=PACK)
+            cut = PACK - GPSIMD_BLOCKS
+            nc.gpsimd.tensor_tensor(
+                out=sq[:, 1, cut:], in0=k_kp[:, 1, cut:], in1=k_kp[:, 1, cut:], op=ALU.mult
+            )
+            nc.scalar.activation(out=sq[:, 0], in_=k_kp[:, 0], func=ACT.Square)
+            nc.scalar.activation(out=sq[:, 1, 0:cut], in_=k_kp[:, 1, 0:cut], func=ACT.Square)
+            natural_squares[j] = sq
+
+        def transpose_sums(j):
             s_ps = sum_psum.tile([P, PACK, P], F32)
             for k in range(PACK):
-                for g in range(terms):
+                for g in range(2):
                     nc.tensor.matmul(
                         out=s_ps[:, k, :],
-                        lhsT=squares[j][:, t, g * F + k * P : g * F + (k + 1) * P],
+                        lhsT=natural_squares[j][:, g, k, :],
                         rhs=ident_f32[:],
                         is_transpose=True,
                         start=(g == 0),
-                        stop=(g == terms - 1),
+                        stop=(g == 1),
                     )
-            sums[(j, t)] = s_ps
+            sums[j] = s_ps
 
         def root_magnitudes(j):
             mg = mag_pool.tile([P, TILES, P, PACK], BF16, align_bytes=64)
-            for t in range(TILES):
-                nc.scalar.activation(
-                    out=mg[:, t, :, :],
-                    in_=sums[(j, t)][:].rearrange("p k n -> p n k"),
-                    func=ACT.Sqrt,
-                    bias=eps_col[:, 0:1],
-                )
+            nc.scalar.activation(
+                out=mg[:, 1],
+                in_=sums[j][:].rearrange("p k n -> p n k"),
+                func=ACT.Sqrt,
+                bias=eps_col[:, 0:1],
+            )
+            nc.scalar.activation(
+                out=mg[:, 0],
+                in_=grouped_squares[j][:, 0],
+                func=ACT.Sqrt,
+                bias=eps_col[:, 0:1],
+            )
             mags[j] = mg
 
         def quantise_magnitudes(j):
@@ -165,32 +184,32 @@ def tile_module2network_t_kernel(tc, K, reference_angles, probes, u_weights, k_b
             )
             mag_codes[j] = (mc, ms)
 
-        def multiply(j, t):
+        def multiply(j):
             kc, ks = key_codes[j]
             mc, ms = mag_codes[j]
-            if t == 0:
-                acc = acc_psum.tile([P, TILES, B], F32)
-                accs[j] = acc
-            for g in range(2):
-                key_cols = slice((g * TILES + t) * P, (g * TILES + t + 1) * P)
+            acc = acc_psum.tile([P, TILES, B], F32)
+            accs[j] = acc
+            for t in range(TILES):
+                for g in range(2):
+                    key_cols = slice((g * TILES + t) * P, (g * TILES + t + 1) * P)
+                    nc.tensor.matmul_mx(
+                        out=acc[:, t, :],
+                        lhsT=kc[:, key_cols].bitcast(FP8X4),
+                        lhsT_scale=ks[:, key_cols],
+                        rhs=rot_codes[:, g * B : (g + 1) * B].bitcast(FP8X4),
+                        rhs_scale=rot_scales[:, g * B : (g + 1) * B],
+                        start=(g == 0),
+                        stop=False,
+                    )
                 nc.tensor.matmul_mx(
-                    out=accs[j][:, t, :],
-                    lhsT=kc[:, key_cols].bitcast(FP8X4),
-                    lhsT_scale=ks[:, key_cols],
-                    rhs=rot_codes[:, g * B : (g + 1) * B].bitcast(FP8X4),
-                    rhs_scale=rot_scales[:, g * B : (g + 1) * B],
-                    start=(g == 0),
-                    stop=False,
+                    out=acc[:, t, :],
+                    lhsT=mc[:, t * P : (t + 1) * P].bitcast(FP8X4),
+                    lhsT_scale=ms[:, t * P : (t + 1) * P],
+                    rhs=u_codes[:].bitcast(FP8X4),
+                    rhs_scale=u_scales[:],
+                    start=False,
+                    stop=True,
                 )
-            nc.tensor.matmul_mx(
-                out=accs[j][:, t, :],
-                lhsT=mc[:, t * P : (t + 1) * P].bitcast(FP8X4),
-                lhsT_scale=ms[:, t * P : (t + 1) * P],
-                rhs=u_codes[:].bitcast(FP8X4),
-                rhs_scale=u_scales[:],
-                start=False,
-                stop=True,
-            )
 
         def add_bias_and_store(j):
             logits = logit_pool.tile([P, TILES, B], F32)
@@ -319,19 +338,18 @@ def tile_module2network_t_kernel(tc, K, reference_angles, probes, u_weights, k_b
         )
 
         with tc.manual_schedule():
-            for t in range(TILES):
-                transpose_keys(0, t)
-            square_keys(0)
-            for step in range(N_PAIRS + MX_LAG + 1):
-                run(add_odd_tiles, step)
-                run(regroup_keys, step)
-                run(square_keys, step + 1)
-                run(load_keys, step + KEY_BUFS)
-                run(quantise_magnitudes, step - 2)
+            for step in range(N_PAIRS + OUT_LAG + 1):
                 for t in range(TILES):
-                    run(transpose_keys, step + 1, t)
-                    run(transpose_sums, step, t)
-                    run(multiply, step - MX_LAG, t)
-                run(quantise_keys, step)
-                run(root_magnitudes, step - 1)
-                run(add_bias_and_store, step - MX_LAG - 1)
+                    run(transpose_keys, step, t)
+                run(transpose_sums, step - 1)
+                run(multiply, step - MX_LAG)
+                run(regroup_keys, step - 1)
+                run(square_last_keys, step - 1)
+                run(square_grouped, step - 2)
+                run(square_natural, step)
+                run(add_grouped, step - 2)
+                run(root_magnitudes, step - 3)
+                run(quantise_magnitudes, step - 4)
+                run(quantise_keys, step - 2)
+                run(add_bias_and_store, step - OUT_LAG)
+                run(load_keys, step + KEY_BUFS)

@@ -112,14 +112,13 @@ def tile_module2network_t_kernel(tc, K, reference_angles, probes, u_weights, k_b
 
         def square_last_keys(j):
             sq = gsquare_pool.tile([P, 2, P, PACK], F32)
-            transposed = keysT[(j, 0)][:].bitcast(BF16).rearrange("p (g u) (n e) -> p g n u e", u=2, e=2)
-            for g in range(2):
-                nc.vector.tensor_tensor(
-                    out=sq[:, g, VECTOR_FROM:, :].rearrange("p n (u e) -> p n u e", u=2),
-                    in0=transposed[:, g, VECTOR_FROM:],
-                    in1=grouped[j][:, g, 0, VECTOR_FROM:, :].rearrange("p n (u e) -> p n u e", u=2),
-                    op=ALU.mult,
-                )
+            last_keys = grouped[j][:, :, 0, VECTOR_FROM:, :].rearrange("p g n k -> p g (n k)")
+            nc.vector.tensor_tensor(
+                out=sq[:, :, VECTOR_FROM:, :].rearrange("p g n k -> p g (n k)"),
+                in0=last_keys,
+                in1=last_keys,
+                op=ALU.mult,
+            )
             grouped_squares[j] = sq
 
         def square_grouped(j):
@@ -343,13 +342,13 @@ def tile_module2network_t_kernel(tc, K, reference_angles, probes, u_weights, k_b
                     run(transpose_keys, step, t)
                 run(transpose_sums, step - 1)
                 run(multiply, step - MX_LAG)
-                run(regroup_keys, step - 1)
-                run(square_last_keys, step - 1)
-                run(square_grouped, step - 2)
-                run(square_natural, step)
-                run(add_grouped, step - 2)
-                run(root_magnitudes, step - 3)
                 run(quantise_magnitudes, step - 4)
                 run(quantise_keys, step - 2)
+                run(square_last_keys, step - 2)
+                run(square_grouped, step - 2)
+                run(add_grouped, step - 2)
+                run(square_natural, step)
+                run(root_magnitudes, step - 3)
+                run(regroup_keys, step - 1)
                 run(add_bias_and_store, step - OUT_LAG)
                 run(load_keys, step + KEY_BUFS)

@@ -20,7 +20,7 @@ PACK = 4
 TILES = 2
 N_PAIRS = N_KEYS // (TILES * P)
 KEY_BUFS = 6
-GPSIMD_BLOCKS = 2
+VECTOR_BLOCKS = 2
 VECTOR_FROM = 112
 MX_LAG = 5
 OUT_LAG = MX_LAG + 1
@@ -135,8 +135,8 @@ def tile_module2network_t_kernel(tc, K, reference_angles, probes, u_weights, k_b
         def square_natural(j):
             sq = nsquare_pool.tile([P, 2, PACK, P], F32)
             k_kp = keys[j][:, 1, :].rearrange("p (g f k) -> p g k f", g=2, k=PACK)
-            cut = PACK - GPSIMD_BLOCKS
-            nc.gpsimd.tensor_tensor(
+            cut = PACK - VECTOR_BLOCKS
+            nc.vector.tensor_tensor(
                 out=sq[:, 1, cut:], in0=k_kp[:, 1, cut:], in1=k_kp[:, 1, cut:], op=ALU.mult
             )
             nc.scalar.activation(out=sq[:, 0], in_=k_kp[:, 0], func=ACT.Square)
@@ -344,10 +344,10 @@ def tile_module2network_t_kernel(tc, K, reference_angles, probes, u_weights, k_b
                 run(multiply, step - MX_LAG)
                 run(quantise_magnitudes, step - 4)
                 run(quantise_keys, step - 2)
+                run(square_natural, step)
                 run(square_last_keys, step - 2)
                 run(square_grouped, step - 2)
                 run(add_grouped, step - 2)
-                run(square_natural, step)
                 run(root_magnitudes, step - 3)
                 run(regroup_keys, step - 1)
                 run(add_bias_and_store, step - OUT_LAG)

@@ -143,9 +143,11 @@ def tile_module2network_t_kernel(tc, K, reference_angles, probes, u_weights, k_b
             nc.scalar.activation(out=sq[:, 1, 0:cut], in_=k_kp[:, 1, 0:cut], func=ACT.Square)
             natural_squares[j] = sq
 
-        def transpose_sums(j):
-            s_ps = sum_psum.tile([P, PACK, P], F32)
-            for k in range(PACK):
+        def transpose_sums(j, half):
+            if half == 0:
+                sums[j] = sum_psum.tile([P, PACK, P], F32, name="s_ps")
+            s_ps = sums[j]
+            for k in range(2 * half, 2 * half + 2):
                 for g in range(2):
                     nc.tensor.matmul(
                         out=s_ps[:, k, :],
@@ -155,7 +157,6 @@ def tile_module2network_t_kernel(tc, K, reference_angles, probes, u_weights, k_b
                         start=(g == 0),
                         stop=(g == 1),
                     )
-            sums[j] = s_ps
 
         def root_magnitudes(j):
             mg = mag_pool.tile([P, TILES, P, PACK], BF16, align_bytes=64)
@@ -183,32 +184,32 @@ def tile_module2network_t_kernel(tc, K, reference_angles, probes, u_weights, k_b
             )
             mag_codes[j] = (mc, ms)
 
-        def multiply(j):
+        def multiply(j, t):
             kc, ks = key_codes[j]
             mc, ms = mag_codes[j]
-            acc = acc_psum.tile([P, TILES, B], F32)
-            accs[j] = acc
-            for t in range(TILES):
-                for g in range(2):
-                    key_cols = slice((g * TILES + t) * P, (g * TILES + t + 1) * P)
-                    nc.tensor.matmul_mx(
-                        out=acc[:, t, :],
-                        lhsT=kc[:, key_cols].bitcast(FP8X4),
-                        lhsT_scale=ks[:, key_cols],
-                        rhs=rot_codes[:, g * B : (g + 1) * B].bitcast(FP8X4),
-                        rhs_scale=rot_scales[:, g * B : (g + 1) * B],
-                        start=(g == 0),
-                        stop=False,
-                    )
+            if t == 0:
+                accs[j] = acc_psum.tile([P, TILES, B], F32, name="acc")
+            acc = accs[j]
+            for g in range(2):
+                key_cols = slice((g * TILES + t) * P, (g * TILES + t + 1) * P)
                 nc.tensor.matmul_mx(
                     out=acc[:, t, :],
-                    lhsT=mc[:, t * P : (t + 1) * P].bitcast(FP8X4),
-                    lhsT_scale=ms[:, t * P : (t + 1) * P],
-                    rhs=u_codes[:].bitcast(FP8X4),
-                    rhs_scale=u_scales[:],
-                    start=False,
-                    stop=True,
+                    lhsT=kc[:, key_cols].bitcast(FP8X4),
+                    lhsT_scale=ks[:, key_cols],
+                    rhs=rot_codes[:, g * B : (g + 1) * B].bitcast(FP8X4),
+                    rhs_scale=rot_scales[:, g * B : (g + 1) * B],
+                    start=(g == 0),
+                    stop=False,
                 )
+            nc.tensor.matmul_mx(
+                out=acc[:, t, :],
+                lhsT=mc[:, t * P : (t + 1) * P].bitcast(FP8X4),
+                lhsT_scale=ms[:, t * P : (t + 1) * P],
+                rhs=u_codes[:].bitcast(FP8X4),
+                rhs_scale=u_scales[:],
+                start=False,
+                stop=True,
+            )
 
         def add_bias_and_store(j):
             logits = logit_pool.tile([P, TILES, B], F32)
@@ -340,8 +341,8 @@ def tile_module2network_t_kernel(tc, K, reference_angles, probes, u_weights, k_b
             for step in range(N_PAIRS + OUT_LAG + 1):
                 for t in range(TILES):
                     run(transpose_keys, step, t)
-                run(transpose_sums, step - 1)
-                run(multiply, step - MX_LAG)
+                    run(transpose_sums, step - 1, t)
+                    run(multiply, step - MX_LAG, t)
                 run(quantise_magnitudes, step - 4)
                 run(quantise_keys, step - 2)
                 run(square_natural, step)

@@ -20,10 +20,10 @@ PACK = 4
 TILES = 2
 N_PAIRS = N_KEYS // (TILES * P)
 KEY_BUFS = 6
-VECTOR_BLOCKS = 2
-VECTOR_FROM = 112
+VECTOR_FROM = 104
+GPSIMD_FROM = 104
 MX_LAG = 5
-OUT_LAG = MX_LAG + 1
+FIRST_MX_STEP = 9
 
 TWO_PI_HI = 6.28125
 TWO_PI_MID = 0.0019353071693331003189
@@ -40,12 +40,12 @@ def tile_module2network_t_kernel(tc, K, reference_angles, probes, u_weights, k_b
         setup = ctx.enter_context(tc.tile_pool(name="setup", bufs=1))
         setup_tmp = ctx.enter_context(tc.tile_pool(name="setup_tmp", bufs=2))
         key_pool = ctx.enter_context(tc.tile_pool(name="keys", bufs=KEY_BUFS))
-        nsquare_pool = ctx.enter_context(tc.tile_pool(name="natural_squares", bufs=3))
+        nsquare_pool = ctx.enter_context(tc.tile_pool(name="natural_squares", bufs=4))
         gsquare_pool = ctx.enter_context(tc.tile_pool(name="grouped_squares", bufs=4))
         grouped_pool = ctx.enter_context(tc.tile_pool(name="grouped", bufs=4))
-        key_code_pool = ctx.enter_context(tc.tile_pool(name="key_codes", bufs=MX_LAG + 3))
+        key_code_pool = ctx.enter_context(tc.tile_pool(name="key_codes", bufs=10))
         mag_pool = ctx.enter_context(tc.tile_pool(name="mag", bufs=4))
-        mag_code_pool = ctx.enter_context(tc.tile_pool(name="mag_codes", bufs=6))
+        mag_code_pool = ctx.enter_context(tc.tile_pool(name="mag_codes", bufs=8))
         logit_pool = ctx.enter_context(tc.tile_pool(name="logits", bufs=4))
         keyT_psum = ctx.enter_context(tc.psum_pool(name="keyT_psum", bufs=4))
         sum_psum = ctx.enter_context(tc.psum_pool(name="sum_psum", bufs=2))
@@ -54,21 +54,25 @@ def tile_module2network_t_kernel(tc, K, reference_angles, probes, u_weights, k_b
         K_pairs = K.rearrange("(j p t) d -> j p (t d)", p=P, t=TILES)
         out_pairs = out.rearrange("(j p t) b -> j p (t b)", p=P, t=TILES)
 
-        angles = setup.tile([P, PACK], BF16)
-        nc.scalar.dma_start(out=angles[:], in_=reference_angles.rearrange("(p k) -> p k", k=PACK))
-        probes_sb = setup.tile([P, 2, D], BF16)
-        nc.scalar.dma_start(out=probes_sb[:], in_=probes.rearrange("(h p) d -> p h d", p=P))
-        u_sb = setup.tile([P, 2, F], BF16)
-        nc.scalar.dma_start(out=u_sb[:], in_=u_weights.rearrange("(h p) f -> p h f", p=P))
-        bias_rows = const.tile([P, B], BF16)
-        nc.scalar.dma_start(out=bias_rows[:], in_=k_bias.partition_broadcast(P))
-
         ident_f32 = const.tile([P, P], F32)
         make_identity(nc, ident_f32[:])
         ident_bf16 = const.tile([P, P], BF16)
         make_identity(nc, ident_bf16[:])
         eps_col = const.tile([P, 1], F32)
         nc.vector.memset(eps_col[:], EPS)
+        zero_col = const.tile([P, 1], F32)
+        nc.vector.memset(zero_col[:], 0.0)
+        shift = setup.tile([P, 2, PACK], F32)
+        nc.vector.memset(shift[:, 0, :], 0.0)
+        nc.vector.memset(shift[:, 1, :], 0.25)
+        angles = setup.tile([P, PACK], BF16)
+        probes_sb = setup.tile([P, 2, D], BF16)
+        u_sb = setup.tile([P, 2, F], BF16)
+        bias_rows = const.tile([P, B], BF16)
+        u_codes = const.tile([P, B], U32, align_bytes=64)
+        u_scales = const.tile([P, B], U8, align_bytes=64)
+        rot_codes = const.tile([P, 2 * B], U32, align_bytes=64)
+        rot_scales = const.tile([P, 2 * B], U8, align_bytes=64)
 
         keys, keysT, natural_squares, grouped, grouped_squares = {}, {}, {}, {}, {}
         key_codes, sums, mags, mag_codes, accs = {}, {}, {}, {}, {}
@@ -112,13 +116,14 @@ def tile_module2network_t_kernel(tc, K, reference_angles, probes, u_weights, k_b
 
         def square_last_keys(j):
             sq = gsquare_pool.tile([P, 2, P, PACK], F32)
-            last_keys = grouped[j][:, :, 0, VECTOR_FROM:, :].rearrange("p g n k -> p g (n k)")
-            nc.vector.tensor_tensor(
-                out=sq[:, :, VECTOR_FROM:, :].rearrange("p g n k -> p g (n k)"),
-                in0=last_keys,
-                in1=last_keys,
-                op=ALU.mult,
-            )
+            transposed = keysT[(j, 0)][:].bitcast(BF16).rearrange("p (g u) (n e) -> p g n u e", u=2, e=2)
+            for g in range(2):
+                nc.vector.tensor_tensor(
+                    out=sq[:, g, VECTOR_FROM:, :].rearrange("p n (u e) -> p n u e", u=2),
+                    in0=transposed[:, g, VECTOR_FROM:],
+                    in1=grouped[j][:, g, 0, VECTOR_FROM:, :].rearrange("p n (u e) -> p n u e", u=2),
+                    op=ALU.mult,
+                )
             grouped_squares[j] = sq
 
         def square_grouped(j):
@@ -134,14 +139,17 @@ def tile_module2network_t_kernel(tc, K, reference_angles, probes, u_weights, k_b
 
         def square_natural(j):
             sq = nsquare_pool.tile([P, 2, PACK, P], F32)
-            k_kp = keys[j][:, 1, :].rearrange("p (g f k) -> p g k f", g=2, k=PACK)
-            cut = PACK - VECTOR_BLOCKS
-            nc.vector.tensor_tensor(
-                out=sq[:, 1, cut:], in0=k_kp[:, 1, cut:], in1=k_kp[:, 1, cut:], op=ALU.mult
-            )
-            nc.scalar.activation(out=sq[:, 0], in_=k_kp[:, 0], func=ACT.Square)
-            nc.scalar.activation(out=sq[:, 1, 0:cut], in_=k_kp[:, 1, 0:cut], func=ACT.Square)
             natural_squares[j] = sq
+            k_kp = keys[j][:, 1, :].rearrange("p (g f k) -> p g k f", g=2, k=PACK)
+            c = GPSIMD_FROM
+            nc.scalar.activation(out=sq[:, :, :, 0:c], in_=k_kp[:, :, :, 0:c], func=ACT.Square)
+
+        def square_natural_rest(j):
+            k_kp = keys[j][:, 1, :].rearrange("p (g f k) -> p g k f", g=2, k=PACK)
+            c = GPSIMD_FROM
+            nc.gpsimd.tensor_tensor(
+                out=natural_squares[j][:, :, :, c:], in0=k_kp[:, :, :, c:], in1=k_kp[:, :, :, c:], op=ALU.mult
+            )
 
         def transpose_sums(j, half):
             if half == 0:
@@ -225,84 +233,95 @@ def tile_module2network_t_kernel(tc, K, reference_angles, probes, u_weights, k_b
             if 0 <= j < N_PAIRS:
                 stage(j, *tile_index)
 
-        for j in range(KEY_BUFS):
-            load_keys(j)
+        setup_tiles = {}
 
-        uT = acc_psum.tile([P, PACK, B], BF16, tag="acc")
-        for h in range(2):
-            for k in range(PACK):
-                nc.tensor.transpose(
-                    uT[:, k, h * P : (h + 1) * P], u_sb[:, h, k::PACK], ident_bf16[:]
-                )
-        u_grouped = setup.tile([P, B, PACK], BF16, align_bytes=64)
-        nc.vector.tensor_copy(out=u_grouped[:], in_=uT[:].rearrange("p k b -> p b k"))
-        u_codes = const.tile([P, B], U32, align_bytes=64)
-        u_scales = const.tile([P, B], U8, align_bytes=64)
-        nc.vector.quantize_mx(
-            out=u_codes[:].bitcast(FP8X4),
-            scales=u_scales[:],
-            in_=u_grouped[:].rearrange("p b k -> p (b k)"),
-        )
+        def transpose_u():
+            uT = acc_psum.tile([P, PACK, B], BF16, tag="acc")
+            setup_tiles["uT"] = uT
+            for h in range(2):
+                for k in range(PACK):
+                    nc.tensor.transpose(uT[:, k, h * P : (h + 1) * P], u_sb[:, h, k::PACK], ident_bf16[:])
 
-        shift = setup.tile([P, 2, PACK], F32)
-        nc.vector.memset(shift[:, 0, :], 0.0)
-        nc.vector.memset(shift[:, 1, :], 0.25)
-        theta = setup.tile([P, 2, PACK], F32)
-        nc.vector.tensor_copy(out=theta[:], in_=angles[:].unsqueeze(1).to_broadcast([P, 2, PACK]))
-        turns = setup.tile([P, 2, PACK], F32)
-        nc.vector.scalar_tensor_tensor(
-            out=turns[:], in0=theta[:], scalar=INV_TWO_PI, in1=shift[:], op0=ALU.mult, op1=ALU.add
-        )
-        whole = setup.tile([P, 2, PACK], F32)
-        nc.vector.tensor_scalar_add(out=whole[:], in0=turns[:], scalar1=ROUND_MAGIC)
-        q = setup.tile([P, 2, PACK], F32)
-        nc.vector.scalar_tensor_tensor(
-            out=q[:], in0=whole[:], scalar=ROUND_MAGIC, in1=shift[:], op0=ALU.subtract, op1=ALU.subtract
-        )
-        reduced_a = setup.tile([P, 2, PACK], F32)
-        nc.vector.scalar_tensor_tensor(
-            out=reduced_a[:], in0=q[:], scalar=-TWO_PI_HI, in1=theta[:], op0=ALU.mult, op1=ALU.add
-        )
-        reduced_b = setup.tile([P, 2, PACK], F32)
-        nc.vector.scalar_tensor_tensor(
-            out=reduced_b[:], in0=q[:], scalar=-TWO_PI_MID, in1=reduced_a[:], op0=ALU.mult, op1=ALU.add
-        )
-        reduced_c = setup.tile([P, 2, PACK], F32)
-        nc.vector.scalar_tensor_tensor(
-            out=reduced_c[:], in0=q[:], scalar=-TWO_PI_LO, in1=reduced_b[:], op0=ALU.mult, op1=ALU.add
-        )
-        reduced = setup.tile([P, 2, PACK], F32)
-        nc.vector.tensor_scalar(
-            out=reduced[:], in0=reduced_c[:], scalar1=PI_BELOW, scalar2=-PI_BELOW, op0=ALU.min, op1=ALU.max
-        )
+        def quantise_u():
+            u_grouped = setup.tile([P, B, PACK], BF16, align_bytes=64)
+            nc.vector.tensor_copy(out=u_grouped[:], in_=setup_tiles["uT"][:].rearrange("p k b -> p b k"))
+            nc.vector.quantize_mx(
+                out=u_codes[:].bitcast(FP8X4),
+                scales=u_scales[:],
+                in_=u_grouped[:].rearrange("p b k -> p (b k)"),
+            )
+
+        def reduce_angles():
+            theta = setup.tile([P, 2, PACK], F32)
+            nc.vector.tensor_copy(out=theta[:], in_=angles[:].unsqueeze(1).to_broadcast([P, 2, PACK]))
+            turns = setup.tile([P, 2, PACK], F32)
+            nc.vector.scalar_tensor_tensor(
+                out=turns[:], in0=theta[:], scalar=INV_TWO_PI, in1=shift[:], op0=ALU.mult, op1=ALU.add
+            )
+            whole = setup.tile([P, 2, PACK], F32)
+            nc.vector.tensor_scalar_add(out=whole[:], in0=turns[:], scalar1=ROUND_MAGIC)
+            q = setup.tile([P, 2, PACK], F32)
+            nc.vector.scalar_tensor_tensor(
+                out=q[:], in0=whole[:], scalar=ROUND_MAGIC, in1=shift[:], op0=ALU.subtract, op1=ALU.subtract
+            )
+            reduced_a = setup.tile([P, 2, PACK], F32)
+            nc.vector.scalar_tensor_tensor(
+                out=reduced_a[:], in0=q[:], scalar=-TWO_PI_HI, in1=theta[:], op0=ALU.mult, op1=ALU.add
+            )
+            reduced_b = setup.tile([P, 2, PACK], F32)
+            nc.vector.scalar_tensor_tensor(
+                out=reduced_b[:], in0=q[:], scalar=-TWO_PI_MID, in1=reduced_a[:], op0=ALU.mult, op1=ALU.add
+            )
+            reduced_c = setup.tile([P, 2, PACK], F32)
+            nc.vector.scalar_tensor_tensor(
+                out=reduced_c[:], in0=q[:], scalar=-TWO_PI_LO, in1=reduced_b[:], op0=ALU.mult, op1=ALU.add
+            )
+            reduced = setup.tile([P, 2, PACK], F32)
+            nc.vector.tensor_scalar(
+                out=reduced[:], in0=reduced_c[:], scalar1=PI_BELOW, scalar2=-PI_BELOW, op0=ALU.min, op1=ALU.max
+            )
+            setup_tiles["reduced"] = reduced
+
         sin_cos = setup.tile([P, 2, PACK], F32)
-        nc.scalar.activation(out=sin_cos[:], in_=reduced[:], func=ACT.Sin)
 
-        squared_probes = setup.tile([P, 2, D], BF16)
-        norm_sq = setup.tile([P, 2], F32)
-        for h in range(2):
-            nc.scalar.activation(
-                out=squared_probes[:, h, :],
-                in_=probes_sb[:, h, :],
-                func=ACT.Square,
-                accum_out=norm_sq[:, h : h + 1],
-            )
-        norm = setup.tile([P, 2], F32)
-        nc.scalar.activation(out=norm[:], in_=norm_sq[:], func=ACT.Sqrt)
-        norm_eps = setup.tile([P, 2], F32)
-        nc.vector.tensor_scalar_add(out=norm_eps[:], in0=norm[:], scalar1=EPS)
-        inv_norm = setup.tile([P, 2], F32)
-        nc.vector.reciprocal(out=inv_norm[:], in_=norm_eps[:])
-        unit = setup.tile([P, 2, D], F32)
-        for h in range(2):
-            nc.vector.tensor_scalar_mul(
-                out=unit[:, h, :], in0=probes_sb[:, h, :], scalar1=inv_norm[:, h : h + 1]
-            )
-        unit_blocks = unit[:].rearrange("b h (g p k) -> b h g k p", g=2, k=PACK)
+        def square_probes():
+            squared_probes = setup.tile([P, 2, D], BF16)
+            norm_sq = setup.tile([P, 2], F32)
+            for h in range(2):
+                nc.scalar.activation(
+                    out=squared_probes[:, h, :],
+                    in_=probes_sb[:, h, :],
+                    func=ACT.Square,
+                    accum_out=norm_sq[:, h : h + 1],
+                )
+            norm = setup.tile([P, 2], F32)
+            nc.scalar.activation(out=norm[:], in_=norm_sq[:], func=ACT.Sqrt)
+            setup_tiles["norm"] = norm
+
+        def normalise_probes():
+            norm_eps = setup.tile([P, 2], F32)
+            nc.vector.tensor_scalar_add(out=norm_eps[:], in0=setup_tiles["norm"][:], scalar1=EPS)
+            inv_norm = setup.tile([P, 2], F32)
+            nc.vector.reciprocal(out=inv_norm[:], in_=norm_eps[:])
+            unit = setup.tile([P, 2, D], F32)
+            for h in range(2):
+                nc.gpsimd.tensor_scalar(
+                    out=unit[:, h, :],
+                    in0=probes_sb[:, h, :],
+                    scalar1=inv_norm[:, h : h + 1],
+                    scalar2=0.0,
+                    op0=ALU.mult,
+                    op1=ALU.add,
+                )
+            setup_tiles["unit"] = unit
+
         planes = setup.tile([P, 2, PACK, B], BF16)
-        for u in range(2):
+
+        def transpose_probes(u):
+            unit_blocks = setup_tiles["unit"][:].rearrange("b h (g p k) -> b h g k p", g=2, k=PACK)
             re_ps = acc_psum.tile([P, 2, B], F32, tag="acc")
             im_ps = acc_psum.tile([P, 2, B], F32, tag="acc")
+            setup_tiles["re"], setup_tiles["im"] = re_ps, im_ps
             for e in range(2):
                 for h in range(2):
                     nc.tensor.transpose(
@@ -311,45 +330,85 @@ def tile_module2network_t_kernel(tc, K, reference_angles, probes, u_weights, k_b
                     nc.tensor.transpose(
                         im_ps[:, e, h * P : (h + 1) * P], unit_blocks[:, h, 1, 2 * u + e, :], ident_f32[:]
                     )
-            for e in range(2):
-                c = 2 * u + e
-                sin_col = sin_cos[:, 0, c : c + 1]
-                cos_col = sin_cos[:, 1, c : c + 1]
-                im_sin = setup_tmp.tile([P, B], F32)
-                nc.vector.tensor_scalar_mul(out=im_sin[:], in0=im_ps[:, e, :], scalar1=sin_col)
-                nc.vector.scalar_tensor_tensor(
-                    out=planes[:, 0, c, :], in0=re_ps[:, e, :], scalar=cos_col, in1=im_sin[:],
-                    op0=ALU.mult, op1=ALU.subtract,
-                )
-                re_sin = setup_tmp.tile([P, B], F32)
-                nc.vector.tensor_scalar_mul(out=re_sin[:], in0=re_ps[:, e, :], scalar1=sin_col)
-                nc.vector.scalar_tensor_tensor(
-                    out=planes[:, 1, c, :], in0=im_ps[:, e, :], scalar=cos_col, in1=re_sin[:],
-                    op0=ALU.mult, op1=ALU.add,
-                )
-        rot_grouped = setup.tile([P, 2, B, PACK], BF16, align_bytes=64)
-        nc.vector.tensor_copy(out=rot_grouped[:], in_=planes[:].rearrange("p g k b -> p g b k"))
-        rot_codes = const.tile([P, 2 * B], U32, align_bytes=64)
-        rot_scales = const.tile([P, 2 * B], U8, align_bytes=64)
-        nc.vector.quantize_mx(
-            out=rot_codes[:].bitcast(FP8X4),
-            scales=rot_scales[:],
-            in_=rot_grouped[:].rearrange("p g b k -> p (g b k)"),
-        )
+
+        def rotate_probes(c):
+            re_ps, im_ps, e = setup_tiles["re"], setup_tiles["im"], c % 2
+            sin_col = sin_cos[:, 0, c : c + 1]
+            cos_col = sin_cos[:, 1, c : c + 1]
+            im_sin = setup_tmp.tile([P, B], F32)
+            nc.vector.tensor_scalar_mul(out=im_sin[:], in0=im_ps[:, e, :], scalar1=sin_col)
+            re_sin = setup_tmp.tile([P, B], F32)
+            nc.vector.tensor_scalar_mul(out=re_sin[:], in0=re_ps[:, e, :], scalar1=sin_col)
+            nc.vector.scalar_tensor_tensor(
+                out=planes[:, 0, c, :], in0=re_ps[:, e, :], scalar=cos_col, in1=im_sin[:],
+                op0=ALU.mult, op1=ALU.subtract,
+            )
+            nc.vector.scalar_tensor_tensor(
+                out=planes[:, 1, c, :], in0=im_ps[:, e, :], scalar=cos_col, in1=re_sin[:],
+                op0=ALU.mult, op1=ALU.add,
+            )
+
+        def quantise_probes():
+            rot_grouped = setup.tile([P, 2, B, PACK], BF16, align_bytes=64)
+            nc.vector.tensor_copy(out=rot_grouped[:], in_=planes[:].rearrange("p g k b -> p g b k"))
+            nc.vector.quantize_mx(
+                out=rot_codes[:].bitcast(FP8X4),
+                scales=rot_scales[:],
+                in_=rot_grouped[:].rearrange("p g b k -> p (g b k)"),
+            )
 
         with tc.manual_schedule():
-            for step in range(N_PAIRS + OUT_LAG + 1):
+            nc.sync.dma_start(out=angles[:], in_=reference_angles.rearrange("(p k) -> p k", k=PACK))
+            load_keys(0)
+            nc.sync.dma_start(out=probes_sb[:], in_=probes.rearrange("(h p) d -> p h d", p=P))
+            load_keys(1)
+            nc.sync.dma_start(out=u_sb[:], in_=u_weights.rearrange("(h p) f -> p h f", p=P))
+            for j in range(2, KEY_BUFS):
+                load_keys(j)
+            nc.sync.dma_start(out=bias_rows[:], in_=k_bias.partition_broadcast(P))
+
+            first_sin = setup.tile([P, 1], F32)
+            nc.scalar.activation(out=first_sin[:], in_=zero_col[:], func=ACT.Sin)
+
+            multiplied, stored = 0, 0
+            for step in range(N_PAIRS + MX_LAG + 2):
+                to_multiply = []
+                if step >= FIRST_MX_STEP:
+                    while multiplied < N_PAIRS and multiplied <= step - MX_LAG and len(to_multiply) < 2:
+                        to_multiply.append(multiplied)
+                        multiplied += 1
                 for t in range(TILES):
                     run(transpose_keys, step, t)
-                    run(transpose_sums, step - 1, t)
-                    run(multiply, step - MX_LAG, t)
+                    run(transpose_sums, step - 2, t)
+                    for j in to_multiply:
+                        multiply(j, t)
+                if step == 1:
+                    transpose_u()
+                if step == 3:
+                    transpose_probes(0)
                 run(quantise_magnitudes, step - 4)
                 run(quantise_keys, step - 2)
-                run(square_natural, step)
-                run(square_last_keys, step - 2)
                 run(square_grouped, step - 2)
                 run(add_grouped, step - 2)
+                run(square_natural, step)
+                run(square_natural_rest, step)
+                if step == 0:
+                    reduce_angles()
+                    nc.scalar.activation(out=sin_cos[:], in_=setup_tiles["reduced"][:], func=ACT.Sin)
+                    square_probes()
                 run(root_magnitudes, step - 3)
                 run(regroup_keys, step - 1)
-                run(add_bias_and_store, step - OUT_LAG)
+                run(square_last_keys, step - 1)
+                if step == 2:
+                    normalise_probes()
+                    quantise_u()
+                if 4 <= step < 4 + PACK:
+                    rotate_probes(step - 4)
+                if step == 5:
+                    transpose_probes(1)
+                if step == 8:
+                    quantise_probes()
+                while stored < multiplied and (stored not in to_multiply):
+                    add_bias_and_store(stored)
+                    stored += 1
                 run(load_keys, step + KEY_BUFS)

@@ -21,7 +21,7 @@ TILES = 2
 N_PAIRS = N_KEYS // (TILES * P)
 KEY_BUFS = 6
 VECTOR_FROM = 104
-GPSIMD_FROM = 104
+GPSIMD_FROM = 96
 MX_LAG = 5
 FIRST_MX_STEP = 9
 
@@ -379,26 +379,28 @@ def tile_module2network_t_kernel(tc, K, reference_angles, probes, u_weights, k_b
                         multiplied += 1
                 for t in range(TILES):
                     run(transpose_keys, step, t)
+                for t in range(TILES):
                     run(transpose_sums, step - 2, t)
-                    for j in to_multiply:
+                for j in to_multiply:
+                    for t in range(TILES):
                         multiply(j, t)
                 if step == 1:
                     transpose_u()
                 if step == 3:
                     transpose_probes(0)
-                run(quantise_magnitudes, step - 4)
-                run(quantise_keys, step - 2)
                 run(square_grouped, step - 2)
-                run(add_grouped, step - 2)
                 run(square_natural, step)
+                run(root_magnitudes, step - 3)
                 run(square_natural_rest, step)
+                run(add_grouped, step - 2)
                 if step == 0:
                     reduce_angles()
                     nc.scalar.activation(out=sin_cos[:], in_=setup_tiles["reduced"][:], func=ACT.Sin)
                     square_probes()
-                run(root_magnitudes, step - 3)
                 run(regroup_keys, step - 1)
                 run(square_last_keys, step - 1)
+                run(quantise_magnitudes, step - 4)
+                run(quantise_keys, step - 2)
                 if step == 2:
                     normalise_probes()
                     quantise_u()

@@ -20,8 +20,7 @@ PACK = 4
 TILES = 2
 N_PAIRS = N_KEYS // (TILES * P)
 KEY_BUFS = 6
-VECTOR_FROM = 104
-GPSIMD_FROM = 96
+VECTOR_FROM = 88
 MX_LAG = 5
 FIRST_MX_STEP = 9
 
@@ -56,8 +55,6 @@ def tile_module2network_t_kernel(tc, K, reference_angles, probes, u_weights, k_b
 
         ident_f32 = const.tile([P, P], F32)
         make_identity(nc, ident_f32[:])
-        ident_bf16 = const.tile([P, P], BF16)
-        make_identity(nc, ident_bf16[:])
         eps_col = const.tile([P, 1], F32)
         nc.vector.memset(eps_col[:], EPS)
         zero_col = const.tile([P, 1], F32)
@@ -79,8 +76,12 @@ def tile_module2network_t_kernel(tc, K, reference_angles, probes, u_weights, k_b
 
         def load_keys(j):
             k_sb = key_pool.tile([P, TILES, D], BF16)
-            nc.sync.dma_start(out=k_sb[:].rearrange("p t d -> p (t d)"), in_=K_pairs[j])
             keys[j] = k_sb
+            if j == 0:
+                for t in (1, 0):
+                    nc.sync.dma_start(out=k_sb[:, t, :], in_=K_pairs[0][:, t * D : (t + 1) * D])
+            else:
+                nc.sync.dma_start(out=k_sb[:].rearrange("p t d -> p (t d)"), in_=K_pairs[j])
 
         def transpose_keys(j, t):
             words = keys[j][:].bitcast(F32)
@@ -141,15 +142,7 @@ def tile_module2network_t_kernel(tc, K, reference_angles, probes, u_weights, k_b
             sq = nsquare_pool.tile([P, 2, PACK, P], F32)
             natural_squares[j] = sq
             k_kp = keys[j][:, 1, :].rearrange("p (g f k) -> p g k f", g=2, k=PACK)
-            c = GPSIMD_FROM
-            nc.scalar.activation(out=sq[:, :, :, 0:c], in_=k_kp[:, :, :, 0:c], func=ACT.Square)
-
-        def square_natural_rest(j):
-            k_kp = keys[j][:, 1, :].rearrange("p (g f k) -> p g k f", g=2, k=PACK)
-            c = GPSIMD_FROM
-            nc.gpsimd.tensor_tensor(
-                out=natural_squares[j][:, :, :, c:], in0=k_kp[:, :, :, c:], in1=k_kp[:, :, :, c:], op=ALU.mult
-            )
+            nc.scalar.activation(out=sq[:], in_=k_kp, func=ACT.Square)
 
         def transpose_sums(j, half):
             if half == 0:
@@ -236,15 +229,18 @@ def tile_module2network_t_kernel(tc, K, reference_angles, probes, u_weights, k_b
         setup_tiles = {}
 
         def transpose_u():
-            uT = acc_psum.tile([P, PACK, B], BF16, tag="acc")
+            uT = acc_psum.tile([P, 2, B], F32, tag="acc")
             setup_tiles["uT"] = uT
+            words = u_sb[:].bitcast(F32)
             for h in range(2):
-                for k in range(PACK):
-                    nc.tensor.transpose(uT[:, k, h * P : (h + 1) * P], u_sb[:, h, k::PACK], ident_bf16[:])
+                for u in range(2):
+                    nc.tensor.transpose(uT[:, u, h * P : (h + 1) * P], words[:, h, u::2], ident_f32[:])
 
         def quantise_u():
             u_grouped = setup.tile([P, B, PACK], BF16, align_bytes=64)
-            nc.vector.tensor_copy(out=u_grouped[:], in_=setup_tiles["uT"][:].rearrange("p k b -> p b k"))
+            nc.vector.tensor_copy(
+                out=u_grouped[:].bitcast(F32), in_=setup_tiles["uT"][:].rearrange("p u b -> p b u")
+            )
             nc.vector.quantize_mx(
                 out=u_codes[:].bitcast(FP8X4),
                 scales=u_scales[:],
@@ -350,7 +346,15 @@ def tile_module2network_t_kernel(tc, K, reference_angles, probes, u_weights, k_b
 
         def quantise_probes():
             rot_grouped = setup.tile([P, 2, B, PACK], BF16, align_bytes=64)
-            nc.vector.tensor_copy(out=rot_grouped[:], in_=planes[:].rearrange("p g k b -> p g b k"))
+            for g in range(2):
+                nc.gpsimd.tensor_scalar(
+                    out=rot_grouped[:, g],
+                    in0=planes[:, g].rearrange("p k b -> p b k"),
+                    scalar1=1.0,
+                    scalar2=0.0,
+                    op0=ALU.mult,
+                    op1=ALU.add,
+                )
             nc.vector.quantize_mx(
                 out=rot_codes[:].bitcast(FP8X4),
                 scales=rot_scales[:],
@@ -391,7 +395,6 @@ def tile_module2network_t_kernel(tc, K, reference_angles, probes, u_weights, k_b
                 run(square_grouped, step - 2)
                 run(square_natural, step)
                 run(root_magnitudes, step - 3)
-                run(square_natural_rest, step)
                 run(add_grouped, step - 2)
                 if step == 0:
                     reduce_angles()

@@ -17,12 +17,17 @@ FLOPS = 2 * N_KEYS * B * (D + F)
 
 P = 128
 PACK = 4
-TILES = 2
-N_PAIRS = N_KEYS // (TILES * P)
-KEY_BUFS = 6
-VECTOR_FROM = 88
-MX_LAG = 5
-FIRST_MX_STEP = 9
+TILES = 4
+HALF = 2
+N_QUADS = N_KEYS // (TILES * P)
+KEY_BUFS = 4
+SQUARES = HALF * 2 * P * PACK
+VECTOR_SQUARES = 480
+SETUP_QUADS = 3
+LAST_QUADS = 3
+TRIGGER_SQUARES = 8
+GPSIMD_FROM = 98
+MX_LAG = 4
 
 TWO_PI_HI = 6.28125
 TWO_PI_MID = 0.0019353071693331003189
@@ -39,19 +44,19 @@ def tile_module2network_t_kernel(tc, K, reference_angles, probes, u_weights, k_b
         setup = ctx.enter_context(tc.tile_pool(name="setup", bufs=1))
         setup_tmp = ctx.enter_context(tc.tile_pool(name="setup_tmp", bufs=2))
         key_pool = ctx.enter_context(tc.tile_pool(name="keys", bufs=KEY_BUFS))
-        nsquare_pool = ctx.enter_context(tc.tile_pool(name="natural_squares", bufs=4))
-        gsquare_pool = ctx.enter_context(tc.tile_pool(name="grouped_squares", bufs=4))
-        grouped_pool = ctx.enter_context(tc.tile_pool(name="grouped", bufs=4))
-        key_code_pool = ctx.enter_context(tc.tile_pool(name="key_codes", bufs=10))
-        mag_pool = ctx.enter_context(tc.tile_pool(name="mag", bufs=4))
-        mag_code_pool = ctx.enter_context(tc.tile_pool(name="mag_codes", bufs=8))
-        logit_pool = ctx.enter_context(tc.tile_pool(name="logits", bufs=4))
+        nsquare_pool = ctx.enter_context(tc.tile_pool(name="natural_squares", bufs=3))
+        gsquare_pool = ctx.enter_context(tc.tile_pool(name="grouped_squares", bufs=3))
+        grouped_pool = ctx.enter_context(tc.tile_pool(name="grouped", bufs=3))
+        key_code_pool = ctx.enter_context(tc.tile_pool(name="key_codes", bufs=MX_LAG))
+        mag_pool = ctx.enter_context(tc.tile_pool(name="mag", bufs=3))
+        mag_code_pool = ctx.enter_context(tc.tile_pool(name="mag_codes", bufs=3))
+        logit_pool = ctx.enter_context(tc.tile_pool(name="logits", bufs=6))
         keyT_psum = ctx.enter_context(tc.psum_pool(name="keyT_psum", bufs=4))
         sum_psum = ctx.enter_context(tc.psum_pool(name="sum_psum", bufs=2))
         acc_psum = ctx.enter_context(tc.psum_pool(name="acc_psum", bufs=2))
 
-        K_pairs = K.rearrange("(j p t) d -> j p (t d)", p=P, t=TILES)
-        out_pairs = out.rearrange("(j p t) b -> j p (t b)", p=P, t=TILES)
+        K_quads = K.rearrange("(j p t) d -> j p (t d)", p=P, t=TILES)
+        out_quads = out.rearrange("(j p t) b -> j p (t b)", p=P, t=TILES)
 
         ident_f32 = const.tile([P, P], F32)
         make_identity(nc, ident_f32[:])
@@ -76,16 +81,16 @@ def tile_module2network_t_kernel(tc, K, reference_angles, probes, u_weights, k_b
 
         def load_keys(j):
             k_sb = key_pool.tile([P, TILES, D], BF16)
+            for t in (HALF, 0):
+                nc.sync.dma_start(
+                    out=k_sb[:, t : t + HALF, :].rearrange("p t d -> p (t d)"),
+                    in_=K_quads[j][:, t * D : (t + HALF) * D],
+                )
             keys[j] = k_sb
-            if j == 0:
-                for t in (1, 0):
-                    nc.sync.dma_start(out=k_sb[:, t, :], in_=K_pairs[0][:, t * D : (t + 1) * D])
-            else:
-                nc.sync.dma_start(out=k_sb[:].rearrange("p t d -> p (t d)"), in_=K_pairs[j])
 
         def transpose_keys(j, t):
             words = keys[j][:].bitcast(F32)
-            kT = keyT_psum.tile([P, PACK, P], F32)
+            kT = keyT_psum.tile([P, PACK, P], F32, tag="kT")
             for g in range(2):
                 for u in range(2):
                     nc.tensor.transpose(
@@ -95,15 +100,14 @@ def tile_module2network_t_kernel(tc, K, reference_angles, probes, u_weights, k_b
                     )
             keysT[(j, t)] = kT
 
-        def regroup_keys(j):
-            kg = grouped_pool.tile([P, 2, TILES, P, PACK], BF16, align_bytes=64)
-            kg_words = kg[:].bitcast(F32)
-            for t in range(TILES):
-                nc.vector.tensor_copy(
-                    out=kg_words[:, :, t, :, :],
-                    in_=keysT[(j, t)][:].rearrange("p (g u) n -> p g n u", u=2),
-                )
-            grouped[j] = kg
+        def regroup_keys(j, t):
+            if j not in grouped:
+                grouped[j] = grouped_pool.tile([P, TILES, 2, P, PACK], BF16, align_bytes=64, name="kg")
+            kg_words = grouped[j][:].bitcast(F32)
+            nc.vector.tensor_copy(
+                out=kg_words[:, t],
+                in_=keysT[(j, t)][:].rearrange("p (g u) n -> p g n u", u=2),
+            )
 
         def quantise_keys(j):
             kc = key_code_pool.tile([P, 2 * TILES * P], U32, align_bytes=64)
@@ -111,69 +115,93 @@ def tile_module2network_t_kernel(tc, K, reference_angles, probes, u_weights, k_b
             nc.vector.quantize_mx(
                 out=kc[:].bitcast(FP8X4),
                 scales=ks[:],
-                in_=grouped[j][:].rearrange("p g t n k -> p (g t n k)"),
+                in_=grouped[j][:].rearrange("p t g n k -> p (t g n k)"),
             )
             key_codes[j] = (kc, ks)
 
+        def vector_squares(j):
+            return SETUP_QUADS <= j < N_QUADS - LAST_QUADS
+
         def square_last_keys(j):
-            sq = gsquare_pool.tile([P, 2, P, PACK], F32)
-            transposed = keysT[(j, 0)][:].bitcast(BF16).rearrange("p (g u) (n e) -> p g n u e", u=2, e=2)
-            for g in range(2):
-                nc.vector.tensor_tensor(
-                    out=sq[:, g, VECTOR_FROM:, :].rearrange("p n (u e) -> p n u e", u=2),
-                    in0=transposed[:, g, VECTOR_FROM:],
-                    in1=grouped[j][:, g, 0, VECTOR_FROM:, :].rearrange("p n (u e) -> p n u e", u=2),
-                    op=ALU.mult,
-                )
+            sq = gsquare_pool.tile([P, HALF, 2, P, PACK], F32)
             grouped_squares[j] = sq
+            if not vector_squares(j):
+                return
+            n0, n1 = P - VECTOR_SQUARES // PACK, P - TRIGGER_SQUARES // PACK
+            transposed = keysT[(j, 1)][:].bitcast(BF16).rearrange("p (g u) (n e) -> p g n u e", u=2, e=2)
+            nc.vector.tensor_tensor(
+                out=sq[:, 1, 1, n0:n1, :].rearrange("p n (u e) -> p n u e", u=2),
+                in0=transposed[:, 1, n0:n1],
+                in1=grouped[j][:, 1, 1, n0:n1, :].rearrange("p n (u e) -> p n u e", u=2),
+                op=ALU.mult,
+            )
+
+        def square_trigger(j):
+            n1 = P - TRIGGER_SQUARES // PACK
+            few = grouped[j][:, 1, 1, n1:, :]
+            nc.vector.tensor_tensor(out=grouped_squares[j][:, 1, 1, n1:, :], in0=few, in1=few, op=ALU.mult)
 
         def square_grouped(j):
+            cut = SQUARES - (VECTOR_SQUARES if vector_squares(j) else TRIGGER_SQUARES)
             nc.scalar.activation(
-                out=grouped_squares[j][:, :, 0:VECTOR_FROM, :].rearrange("p g n k -> p g (n k)"),
-                in_=grouped[j][:, :, 0, 0:VECTOR_FROM, :].rearrange("p g n k -> p g (n k)"),
+                out=grouped_squares[j][:].rearrange("p t g n k -> p (t g n k)")[:, 0:cut],
+                in_=grouped[j][:].rearrange("p t g n k -> p (t g n k)")[:, 0:cut],
                 func=ACT.Square,
             )
 
-        def add_grouped(j):
+        def add_grouped(j, engine):
             sq = grouped_squares[j]
-            nc.gpsimd.tensor_tensor(out=sq[:, 0], in0=sq[:, 0], in1=sq[:, 1], op=ALU.add)
+            engine.tensor_tensor(out=sq[:, :, 0], in0=sq[:, :, 0], in1=sq[:, :, 1], op=ALU.add)
+
+        def natural_views(j):
+            k_kp = keys[j][:, HALF:, :].rearrange("p t (g f k) -> p (t g) k f", g=2, k=PACK)
+            return k_kp, natural_squares[j][:].rearrange("p t g k f -> p (t g) k f")
 
         def square_natural(j):
-            sq = nsquare_pool.tile([P, 2, PACK, P], F32)
-            natural_squares[j] = sq
-            k_kp = keys[j][:, 1, :].rearrange("p (g f k) -> p g k f", g=2, k=PACK)
-            nc.scalar.activation(out=sq[:], in_=k_kp, func=ACT.Square)
+            natural_squares[j] = nsquare_pool.tile([P, HALF, 2, PACK, P], F32, name="nsq")
+            k_kp, sq_kp = natural_views(j)
+            c = GPSIMD_FROM
+            nc.scalar.activation(out=sq_kp[:, :, :, 0:c], in_=k_kp[:, :, :, 0:c], func=ACT.Square)
 
-        def transpose_sums(j, half):
-            if half == 0:
-                sums[j] = sum_psum.tile([P, PACK, P], F32, name="s_ps")
-            s_ps = sums[j]
-            for k in range(2 * half, 2 * half + 2):
+        def square_natural_rest(j):
+            k_kp, sq_kp = natural_views(j)
+            c = GPSIMD_FROM
+            nc.gpsimd.tensor_tensor(
+                out=sq_kp[:, :, :, c:], in0=k_kp[:, :, :, c:], in1=k_kp[:, :, :, c:], op=ALU.mult
+            )
+
+        def transpose_sums(j, t):
+            s_ps = sum_psum.tile([P, PACK, P], F32)
+            for k in range(PACK):
                 for g in range(2):
                     nc.tensor.matmul(
                         out=s_ps[:, k, :],
-                        lhsT=natural_squares[j][:, g, k, :],
+                        lhsT=natural_squares[j][:, t, g, k, :],
                         rhs=ident_f32[:],
                         is_transpose=True,
                         start=(g == 0),
                         stop=(g == 1),
                     )
+            sums[(j, t)] = s_ps
 
-        def root_magnitudes(j):
+        def root_natural(j):
             mg = mag_pool.tile([P, TILES, P, PACK], BF16, align_bytes=64)
-            nc.scalar.activation(
-                out=mg[:, 1],
-                in_=sums[j][:].rearrange("p k n -> p n k"),
-                func=ACT.Sqrt,
-                bias=eps_col[:, 0:1],
-            )
-            nc.scalar.activation(
-                out=mg[:, 0],
-                in_=grouped_squares[j][:, 0],
-                func=ACT.Sqrt,
-                bias=eps_col[:, 0:1],
-            )
             mags[j] = mg
+            for t in range(HALF):
+                nc.scalar.activation(
+                    out=mg[:, HALF + t],
+                    in_=sums[(j, t)][:].rearrange("p k n -> p n k"),
+                    func=ACT.Sqrt,
+                    bias=eps_col[:, 0:1],
+                )
+
+        def root_grouped(j):
+            nc.scalar.activation(
+                out=mags[j][:, 0:HALF].rearrange("p t n k -> p t (n k)"),
+                in_=grouped_squares[j][:, :, 0].rearrange("p t n k -> p t (n k)"),
+                func=ACT.Sqrt,
+                bias=eps_col[:, 0:1],
+            )
 
         def quantise_magnitudes(j):
             mc = mag_code_pool.tile([P, TILES * P], U32, align_bytes=64)
@@ -188,13 +216,17 @@ def tile_module2network_t_kernel(tc, K, reference_angles, probes, u_weights, k_b
         def multiply(j, t):
             kc, ks = key_codes[j]
             mc, ms = mag_codes[j]
-            if t == 0:
-                accs[j] = acc_psum.tile([P, TILES, B], F32, name="acc")
-            acc = accs[j]
+            if t % 2 == 0:
+                if j < N_QUADS - MX_LAG:
+                    products = acc_psum.tile([P, 2, B], F32, tag="acc")
+                else:
+                    products = keyT_psum.tile([P, 2, B], F32, tag="kT")
+                accs[(j, t // 2)] = products
+            acc = accs[(j, t // 2)][:, t % 2, :]
             for g in range(2):
-                key_cols = slice((g * TILES + t) * P, (g * TILES + t + 1) * P)
+                key_cols = slice((2 * t + g) * P, (2 * t + g + 1) * P)
                 nc.tensor.matmul_mx(
-                    out=acc[:, t, :],
+                    out=acc,
                     lhsT=kc[:, key_cols].bitcast(FP8X4),
                     lhsT_scale=ks[:, key_cols],
                     rhs=rot_codes[:, g * B : (g + 1) * B].bitcast(FP8X4),
@@ -203,7 +235,7 @@ def tile_module2network_t_kernel(tc, K, reference_angles, probes, u_weights, k_b
                     stop=False,
                 )
             nc.tensor.matmul_mx(
-                out=acc[:, t, :],
+                out=acc,
                 lhsT=mc[:, t * P : (t + 1) * P].bitcast(FP8X4),
                 lhsT_scale=ms[:, t * P : (t + 1) * P],
                 rhs=u_codes[:].bitcast(FP8X4),
@@ -212,18 +244,21 @@ def tile_module2network_t_kernel(tc, K, reference_angles, probes, u_weights, k_b
                 stop=True,
             )
 
-        def add_bias_and_store(j):
-            logits = logit_pool.tile([P, TILES, B], F32)
+        def add_bias_and_store(j, pair):
+            logits = logit_pool.tile([P, 2, B], F32)
             nc.vector.tensor_tensor(
                 out=logits[:],
-                in0=accs[j][:],
-                in1=bias_rows[:].unsqueeze(1).to_broadcast([P, TILES, B]),
+                in0=accs[(j, pair)][:],
+                in1=bias_rows[:].unsqueeze(1).to_broadcast([P, 2, B]),
                 op=ALU.add,
             )
-            nc.sync.dma_start(out=out_pairs[j], in_=logits[:].rearrange("p t b -> p (t b)"))
+            nc.sync.dma_start(
+                out=out_quads[j][:, 2 * pair * B : 2 * (pair + 1) * B],
+                in_=logits[:].rearrange("p t b -> p (t b)"),
+            )
 
         def run(stage, j, *tile_index):
-            if 0 <= j < N_PAIRS:
+            if 0 <= j < N_QUADS:
                 stage(j, *tile_index)
 
         setup_tiles = {}
@@ -327,34 +362,30 @@ def tile_module2network_t_kernel(tc, K, reference_angles, probes, u_weights, k_b
                         im_ps[:, e, h * P : (h + 1) * P], unit_blocks[:, h, 1, 2 * u + e, :], ident_f32[:]
                     )
 
+        sine_products = {}
+
+        def scale_by_sines(c):
+            for name, part in (("im", setup_tiles["im"]), ("re", setup_tiles["re"])):
+                scaled = setup_tmp.tile([P, B], F32, name=name + "_sin")
+                nc.scalar.activation(
+                    out=scaled[:], in_=part[:, c % 2, :], func=ACT.Copy, scale=sin_cos[:, 0, c : c + 1]
+                )
+                sine_products[(name, c)] = scaled
+
         def rotate_probes(c):
-            re_ps, im_ps, e = setup_tiles["re"], setup_tiles["im"], c % 2
-            sin_col = sin_cos[:, 0, c : c + 1]
             cos_col = sin_cos[:, 1, c : c + 1]
-            im_sin = setup_tmp.tile([P, B], F32)
-            nc.vector.tensor_scalar_mul(out=im_sin[:], in0=im_ps[:, e, :], scalar1=sin_col)
-            re_sin = setup_tmp.tile([P, B], F32)
-            nc.vector.tensor_scalar_mul(out=re_sin[:], in0=re_ps[:, e, :], scalar1=sin_col)
             nc.vector.scalar_tensor_tensor(
-                out=planes[:, 0, c, :], in0=re_ps[:, e, :], scalar=cos_col, in1=im_sin[:],
-                op0=ALU.mult, op1=ALU.subtract,
+                out=planes[:, 0, c, :], in0=setup_tiles["re"][:, c % 2, :], scalar=cos_col,
+                in1=sine_products[("im", c)][:], op0=ALU.mult, op1=ALU.subtract,
             )
             nc.vector.scalar_tensor_tensor(
-                out=planes[:, 1, c, :], in0=im_ps[:, e, :], scalar=cos_col, in1=re_sin[:],
-                op0=ALU.mult, op1=ALU.add,
+                out=planes[:, 1, c, :], in0=setup_tiles["im"][:, c % 2, :], scalar=cos_col,
+                in1=sine_products[("re", c)][:], op0=ALU.mult, op1=ALU.add,
             )
 
         def quantise_probes():
             rot_grouped = setup.tile([P, 2, B, PACK], BF16, align_bytes=64)
-            for g in range(2):
-                nc.gpsimd.tensor_scalar(
-                    out=rot_grouped[:, g],
-                    in0=planes[:, g].rearrange("p k b -> p b k"),
-                    scalar1=1.0,
-                    scalar2=0.0,
-                    op0=ALU.mult,
-                    op1=ALU.add,
-                )
+            nc.vector.tensor_copy(out=rot_grouped[:], in_=planes[:].rearrange("p g k b -> p g b k"))
             nc.vector.quantize_mx(
                 out=rot_codes[:].bitcast(FP8X4),
                 scales=rot_scales[:],
@@ -365,55 +396,68 @@ def tile_module2network_t_kernel(tc, K, reference_angles, probes, u_weights, k_b
             nc.sync.dma_start(out=angles[:], in_=reference_angles.rearrange("(p k) -> p k", k=PACK))
             load_keys(0)
             nc.sync.dma_start(out=probes_sb[:], in_=probes.rearrange("(h p) d -> p h d", p=P))
-            load_keys(1)
             nc.sync.dma_start(out=u_sb[:], in_=u_weights.rearrange("(h p) f -> p h f", p=P))
-            for j in range(2, KEY_BUFS):
+            for j in range(1, KEY_BUFS):
                 load_keys(j)
             nc.sync.dma_start(out=bias_rows[:], in_=k_bias.partition_broadcast(P))
 
             first_sin = setup.tile([P, 1], F32)
             nc.scalar.activation(out=first_sin[:], in_=zero_col[:], func=ACT.Sin)
 
-            multiplied, stored = 0, 0
-            for step in range(N_PAIRS + MX_LAG + 2):
-                to_multiply = []
-                if step >= FIRST_MX_STEP:
-                    while multiplied < N_PAIRS and multiplied <= step - MX_LAG and len(to_multiply) < 2:
-                        to_multiply.append(multiplied)
-                        multiplied += 1
-                for t in range(TILES):
-                    run(transpose_keys, step, t)
-                for t in range(TILES):
-                    run(transpose_sums, step - 2, t)
-                for j in to_multiply:
-                    for t in range(TILES):
-                        multiply(j, t)
-                if step == 1:
-                    transpose_u()
-                if step == 3:
-                    transpose_probes(0)
+            for step in range(N_QUADS + MX_LAG + 2):
                 run(square_grouped, step - 2)
+                if step == 3:
+                    for c in (2, 3):
+                        scale_by_sines(c)
+                run(root_natural, step - 3)
+                run(root_grouped, step - 3)
                 run(square_natural, step)
-                run(root_magnitudes, step - 3)
-                run(add_grouped, step - 2)
+                if step == 2:
+                    for c in (0, 1):
+                        scale_by_sines(c)
                 if step == 0:
                     reduce_angles()
                     nc.scalar.activation(out=sin_cos[:], in_=setup_tiles["reduced"][:], func=ACT.Sin)
                     square_probes()
-                run(regroup_keys, step - 1)
+                for t in (HALF, HALF + 1, 1, 0):
+                    run(regroup_keys, step - 1, t)
                 run(square_last_keys, step - 1)
-                run(quantise_magnitudes, step - 4)
-                run(quantise_keys, step - 2)
-                if step == 2:
-                    normalise_probes()
+                if step < N_QUADS:
+                    for pair in range(2):
+                        run(add_bias_and_store, step - MX_LAG - 1, pair)
+                    run(quantise_magnitudes, step - 4)
+                    run(quantise_keys, step - 2)
+                    run(square_trigger, step - 2)
+                    run(add_grouped, step - 2, nc.gpsimd)
+                    run(square_natural_rest, step)
+                else:
+                    run(square_trigger, step - 2)
+                    run(add_grouped, step - 2, nc.vector)
+                    run(quantise_magnitudes, step - 4)
+                    run(quantise_keys, step - 2)
+                    for pair in range(2):
+                        run(add_bias_and_store, step - MX_LAG - 1, pair)
+                if step == 1:
+                    transpose_u()
                     quantise_u()
-                if 4 <= step < 4 + PACK:
-                    rotate_probes(step - 4)
-                if step == 5:
-                    transpose_probes(1)
-                if step == 8:
+                    normalise_probes()
+                if step == 2:
+                    for c in (0, 1):
+                        rotate_probes(c)
+                if step == 3:
+                    for c in (2, 3):
+                        rotate_probes(c)
                     quantise_probes()
-                while stored < multiplied and (stored not in to_multiply):
-                    add_bias_and_store(stored)
-                    stored += 1
+                for t in (HALF, HALF + 1):
+                    run(transpose_keys, step, t)
+                for t in range(HALF):
+                    run(transpose_sums, step - 2, t)
+                for t in (0, 1):
+                    run(multiply, step - MX_LAG, t)
+                for t in (1, 0):
+                    run(transpose_keys, step, t)
+                for t in (2, 3):
+                    run(multiply, step - MX_LAG, t)
+                if step in (1, 2):
+                    transpose_probes(step - 1)
                 run(load_keys, step + KEY_BUFS)

from contextlib import ExitStack

import concourse.mybir as mybir
from concourse.masks import make_identity

F32 = mybir.dt.float32
BF16 = mybir.dt.bfloat16
U32 = mybir.dt.uint32
U8 = mybir.dt.uint8
FP8X4 = mybir.dt.float8_e4m3fn_x4
ACT = mybir.ActivationFunctionType
ALU = mybir.AluOpType

N_KEYS, D, F, B = 12288, 1024, 512, 256
EPS = 1e-8
FLOPS = 2 * N_KEYS * B * (D + F)

P = 128
PACK = 4
TILES = 4
HALF = 2
N_QUADS = N_KEYS // (TILES * P)
KEY_BUFS = 4
SQUARES = HALF * 2 * P * PACK
VECTOR_SQUARES = 480
SETUP_QUADS = 3
LAST_QUADS = 3
TRIGGER_SQUARES = 8
GPSIMD_FROM = 98
MX_LAG = 4

TWO_PI_HI = 6.28125
TWO_PI_MID = 0.0019353071693331003189
TWO_PI_LO = 1.0253131677018245682e-11
INV_TWO_PI = 0.15915493667125701904
ROUND_MAGIC = 12582912.0
PI_BELOW = 3.1415925025939941406


def tile_module2network_t_kernel(tc, K, reference_angles, probes, u_weights, k_bias, out):
    nc = tc.nc
    with ExitStack() as ctx:
        const = ctx.enter_context(tc.tile_pool(name="const", bufs=1))
        setup = ctx.enter_context(tc.tile_pool(name="setup", bufs=1))
        setup_tmp = ctx.enter_context(tc.tile_pool(name="setup_tmp", bufs=2))
        key_pool = ctx.enter_context(tc.tile_pool(name="keys", bufs=KEY_BUFS))
        nsquare_pool = ctx.enter_context(tc.tile_pool(name="natural_squares", bufs=3))
        gsquare_pool = ctx.enter_context(tc.tile_pool(name="grouped_squares", bufs=3))
        grouped_pool = ctx.enter_context(tc.tile_pool(name="grouped", bufs=3))
        key_code_pool = ctx.enter_context(tc.tile_pool(name="key_codes", bufs=MX_LAG))
        mag_pool = ctx.enter_context(tc.tile_pool(name="mag", bufs=3))
        mag_code_pool = ctx.enter_context(tc.tile_pool(name="mag_codes", bufs=3))
        logit_pool = ctx.enter_context(tc.tile_pool(name="logits", bufs=6))
        keyT_psum = ctx.enter_context(tc.psum_pool(name="keyT_psum", bufs=4))
        sum_psum = ctx.enter_context(tc.psum_pool(name="sum_psum", bufs=2))
        acc_psum = ctx.enter_context(tc.psum_pool(name="acc_psum", bufs=2))

        K_quads = K.rearrange("(j p t) d -> j p (t d)", p=P, t=TILES)
        out_quads = out.rearrange("(j p t) b -> j p (t b)", p=P, t=TILES)

        ident_f32 = const.tile([P, P], F32)
        make_identity(nc, ident_f32[:])
        eps_col = const.tile([P, 1], F32)
        nc.vector.memset(eps_col[:], EPS)
        zero_col = const.tile([P, 1], F32)
        nc.vector.memset(zero_col[:], 0.0)
        shift = setup.tile([P, 2, PACK], F32)
        nc.vector.memset(shift[:, 0, :], 0.0)
        nc.vector.memset(shift[:, 1, :], 0.25)
        angles = setup.tile([P, PACK], BF16)
        probes_sb = setup.tile([P, 2, D], BF16)
        u_sb = setup.tile([P, 2, F], BF16)
        bias_rows = const.tile([P, B], BF16)
        u_codes = const.tile([P, B], U32, align_bytes=64)
        u_scales = const.tile([P, B], U8, align_bytes=64)
        rot_codes = const.tile([P, 2 * B], U32, align_bytes=64)
        rot_scales = const.tile([P, 2 * B], U8, align_bytes=64)

        keys, keysT, natural_squares, grouped, grouped_squares = {}, {}, {}, {}, {}
        key_codes, sums, mags, mag_codes, accs = {}, {}, {}, {}, {}

        def load_keys(j):
            k_sb = key_pool.tile([P, TILES, D], BF16)
            for t in (HALF, 0):
                nc.sync.dma_start(
                    out=k_sb[:, t : t + HALF, :].rearrange("p t d -> p (t d)"),
                    in_=K_quads[j][:, t * D : (t + HALF) * D],
                )
            keys[j] = k_sb

        def transpose_keys(j, t):
            words = keys[j][:].bitcast(F32)
            kT = keyT_psum.tile([P, PACK, P], F32, tag="kT")
            for g in range(2):
                for u in range(2):
                    nc.tensor.transpose(
                        kT[:, 2 * g + u, :],
                        words[:, t, 2 * g * P + u : 2 * (g + 1) * P : 2],
                        ident_f32[:],
                    )
            keysT[(j, t)] = kT

        def regroup_keys(j, t):
            if j not in grouped:
                grouped[j] = grouped_pool.tile([P, TILES, 2, P, PACK], BF16, align_bytes=64, name="kg")
            kg_words = grouped[j][:].bitcast(F32)
            nc.vector.tensor_copy(
                out=kg_words[:, t],
                in_=keysT[(j, t)][:].rearrange("p (g u) n -> p g n u", u=2),
            )

        def quantise_keys(j):
            kc = key_code_pool.tile([P, 2 * TILES * P], U32, align_bytes=64)
            ks = key_code_pool.tile([P, 2 * TILES * P], U8, align_bytes=64)
            nc.vector.quantize_mx(
                out=kc[:].bitcast(FP8X4),
                scales=ks[:],
                in_=grouped[j][:].rearrange("p t g n k -> p (t g n k)"),
            )
            key_codes[j] = (kc, ks)

        def vector_squares(j):
            return SETUP_QUADS <= j < N_QUADS - LAST_QUADS

        def square_last_keys(j):
            sq = gsquare_pool.tile([P, HALF, 2, P, PACK], F32)
            grouped_squares[j] = sq
            if not vector_squares(j):
                return
            n0, n1 = P - VECTOR_SQUARES // PACK, P - TRIGGER_SQUARES // PACK
            transposed = keysT[(j, 1)][:].bitcast(BF16).rearrange("p (g u) (n e) -> p g n u e", u=2, e=2)
            nc.vector.tensor_tensor(
                out=sq[:, 1, 1, n0:n1, :].rearrange("p n (u e) -> p n u e", u=2),
                in0=transposed[:, 1, n0:n1],
                in1=grouped[j][:, 1, 1, n0:n1, :].rearrange("p n (u e) -> p n u e", u=2),
                op=ALU.mult,
            )

        def square_trigger(j):
            n1 = P - TRIGGER_SQUARES // PACK
            few = grouped[j][:, 1, 1, n1:, :]
            nc.vector.tensor_tensor(out=grouped_squares[j][:, 1, 1, n1:, :], in0=few, in1=few, op=ALU.mult)

        def square_grouped(j):
            cut = SQUARES - (VECTOR_SQUARES if vector_squares(j) else TRIGGER_SQUARES)
            nc.scalar.activation(
                out=grouped_squares[j][:].rearrange("p t g n k -> p (t g n k)")[:, 0:cut],
                in_=grouped[j][:].rearrange("p t g n k -> p (t g n k)")[:, 0:cut],
                func=ACT.Square,
            )

        def add_grouped(j, engine):
            sq = grouped_squares[j]
            engine.tensor_tensor(out=sq[:, :, 0], in0=sq[:, :, 0], in1=sq[:, :, 1], op=ALU.add)

        def natural_views(j):
            k_kp = keys[j][:, HALF:, :].rearrange("p t (g f k) -> p (t g) k f", g=2, k=PACK)
            return k_kp, natural_squares[j][:].rearrange("p t g k f -> p (t g) k f")

        def square_natural(j):
            natural_squares[j] = nsquare_pool.tile([P, HALF, 2, PACK, P], F32, name="nsq")
            k_kp, sq_kp = natural_views(j)
            c = GPSIMD_FROM
            nc.scalar.activation(out=sq_kp[:, :, :, 0:c], in_=k_kp[:, :, :, 0:c], func=ACT.Square)

        def square_natural_rest(j):
            k_kp, sq_kp = natural_views(j)
            c = GPSIMD_FROM
            nc.gpsimd.tensor_tensor(
                out=sq_kp[:, :, :, c:], in0=k_kp[:, :, :, c:], in1=k_kp[:, :, :, c:], op=ALU.mult
            )

        def transpose_sums(j, t):
            s_ps = sum_psum.tile([P, PACK, P], F32)
            for k in range(PACK):
                for g in range(2):
                    nc.tensor.matmul(
                        out=s_ps[:, k, :],
                        lhsT=natural_squares[j][:, t, g, k, :],
                        rhs=ident_f32[:],
                        is_transpose=True,
                        start=(g == 0),
                        stop=(g == 1),
                    )
            sums[(j, t)] = s_ps

        def root_natural(j):
            mg = mag_pool.tile([P, TILES, P, PACK], BF16, align_bytes=64)
            mags[j] = mg
            for t in range(HALF):
                nc.scalar.activation(
                    out=mg[:, HALF + t],
                    in_=sums[(j, t)][:].rearrange("p k n -> p n k"),
                    func=ACT.Sqrt,
                    bias=eps_col[:, 0:1],
                )

        def root_grouped(j):
            nc.scalar.activation(
                out=mags[j][:, 0:HALF].rearrange("p t n k -> p t (n k)"),
                in_=grouped_squares[j][:, :, 0].rearrange("p t n k -> p t (n k)"),
                func=ACT.Sqrt,
                bias=eps_col[:, 0:1],
            )

        def quantise_magnitudes(j):
            mc = mag_code_pool.tile([P, TILES * P], U32, align_bytes=64)
            ms = mag_code_pool.tile([P, TILES * P], U8, align_bytes=64)
            nc.vector.quantize_mx(
                out=mc[:].bitcast(FP8X4),
                scales=ms[:],
                in_=mags[j][:].rearrange("p t n k -> p (t n k)"),
            )
            mag_codes[j] = (mc, ms)

        def multiply(j, t):
            kc, ks = key_codes[j]
            mc, ms = mag_codes[j]
            if t % 2 == 0:
                if j < N_QUADS - MX_LAG:
                    products = acc_psum.tile([P, 2, B], F32, tag="acc")
                else:
                    products = keyT_psum.tile([P, 2, B], F32, tag="kT")
                accs[(j, t // 2)] = products
            acc = accs[(j, t // 2)][:, t % 2, :]
            for g in range(2):
                key_cols = slice((2 * t + g) * P, (2 * t + g + 1) * P)
                nc.tensor.matmul_mx(
                    out=acc,
                    lhsT=kc[:, key_cols].bitcast(FP8X4),
                    lhsT_scale=ks[:, key_cols],
                    rhs=rot_codes[:, g * B : (g + 1) * B].bitcast(FP8X4),
                    rhs_scale=rot_scales[:, g * B : (g + 1) * B],
                    start=(g == 0),
                    stop=False,
                )
            nc.tensor.matmul_mx(
                out=acc,
                lhsT=mc[:, t * P : (t + 1) * P].bitcast(FP8X4),
                lhsT_scale=ms[:, t * P : (t + 1) * P],
                rhs=u_codes[:].bitcast(FP8X4),
                rhs_scale=u_scales[:],
                start=False,
                stop=True,
            )

        def add_bias_and_store(j, pair):
            logits = logit_pool.tile([P, 2, B], F32)
            nc.vector.tensor_tensor(
                out=logits[:],
                in0=accs[(j, pair)][:],
                in1=bias_rows[:].unsqueeze(1).to_broadcast([P, 2, B]),
                op=ALU.add,
            )
            nc.sync.dma_start(
                out=out_quads[j][:, 2 * pair * B : 2 * (pair + 1) * B],
                in_=logits[:].rearrange("p t b -> p (t b)"),
            )

        def run(stage, j, *tile_index):
            if 0 <= j < N_QUADS:
                stage(j, *tile_index)

        setup_tiles = {}

        def transpose_u():
            uT = acc_psum.tile([P, 2, B], F32, tag="acc")
            setup_tiles["uT"] = uT
            words = u_sb[:].bitcast(F32)
            for h in range(2):
                for u in range(2):
                    nc.tensor.transpose(uT[:, u, h * P : (h + 1) * P], words[:, h, u::2], ident_f32[:])

        def quantise_u():
            u_grouped = setup.tile([P, B, PACK], BF16, align_bytes=64)
            nc.vector.tensor_copy(
                out=u_grouped[:].bitcast(F32), in_=setup_tiles["uT"][:].rearrange("p u b -> p b u")
            )
            nc.vector.quantize_mx(
                out=u_codes[:].bitcast(FP8X4),
                scales=u_scales[:],
                in_=u_grouped[:].rearrange("p b k -> p (b k)"),
            )

        def reduce_angles():
            theta = setup.tile([P, 2, PACK], F32)
            nc.vector.tensor_copy(out=theta[:], in_=angles[:].unsqueeze(1).to_broadcast([P, 2, PACK]))
            turns = setup.tile([P, 2, PACK], F32)
            nc.vector.scalar_tensor_tensor(
                out=turns[:], in0=theta[:], scalar=INV_TWO_PI, in1=shift[:], op0=ALU.mult, op1=ALU.add
            )
            whole = setup.tile([P, 2, PACK], F32)
            nc.vector.tensor_scalar_add(out=whole[:], in0=turns[:], scalar1=ROUND_MAGIC)
            q = setup.tile([P, 2, PACK], F32)
            nc.vector.scalar_tensor_tensor(
                out=q[:], in0=whole[:], scalar=ROUND_MAGIC, in1=shift[:], op0=ALU.subtract, op1=ALU.subtract
            )
            reduced_a = setup.tile([P, 2, PACK], F32)
            nc.vector.scalar_tensor_tensor(
                out=reduced_a[:], in0=q[:], scalar=-TWO_PI_HI, in1=theta[:], op0=ALU.mult, op1=ALU.add
            )
            reduced_b = setup.tile([P, 2, PACK], F32)
            nc.vector.scalar_tensor_tensor(
                out=reduced_b[:], in0=q[:], scalar=-TWO_PI_MID, in1=reduced_a[:], op0=ALU.mult, op1=ALU.add
            )
            reduced_c = setup.tile([P, 2, PACK], F32)
            nc.vector.scalar_tensor_tensor(
                out=reduced_c[:], in0=q[:], scalar=-TWO_PI_LO, in1=reduced_b[:], op0=ALU.mult, op1=ALU.add
            )
            reduced = setup.tile([P, 2, PACK], F32)
            nc.vector.tensor_scalar(
                out=reduced[:], in0=reduced_c[:], scalar1=PI_BELOW, scalar2=-PI_BELOW, op0=ALU.min, op1=ALU.max
            )
            setup_tiles["reduced"] = reduced

        sin_cos = setup.tile([P, 2, PACK], F32)

        def square_probes():
            squared_probes = setup.tile([P, 2, D], BF16)
            norm_sq = setup.tile([P, 2], F32)
            for h in range(2):
                nc.scalar.activation(
                    out=squared_probes[:, h, :],
                    in_=probes_sb[:, h, :],
                    func=ACT.Square,
                    accum_out=norm_sq[:, h : h + 1],
                )
            norm = setup.tile([P, 2], F32)
            nc.scalar.activation(out=norm[:], in_=norm_sq[:], func=ACT.Sqrt)
            setup_tiles["norm"] = norm

        def normalise_probes():
            norm_eps = setup.tile([P, 2], F32)
            nc.vector.tensor_scalar_add(out=norm_eps[:], in0=setup_tiles["norm"][:], scalar1=EPS)
            inv_norm = setup.tile([P, 2], F32)
            nc.vector.reciprocal(out=inv_norm[:], in_=norm_eps[:])
            unit = setup.tile([P, 2, D], F32)
            for h in range(2):
                nc.gpsimd.tensor_scalar(
                    out=unit[:, h, :],
                    in0=probes_sb[:, h, :],
                    scalar1=inv_norm[:, h : h + 1],
                    scalar2=0.0,
                    op0=ALU.mult,
                    op1=ALU.add,
                )
            setup_tiles["unit"] = unit

        planes = setup.tile([P, 2, PACK, B], BF16)

        def transpose_probes(u):
            unit_blocks = setup_tiles["unit"][:].rearrange("b h (g p k) -> b h g k p", g=2, k=PACK)
            re_ps = acc_psum.tile([P, 2, B], F32, tag="acc")
            im_ps = acc_psum.tile([P, 2, B], F32, tag="acc")
            setup_tiles["re"], setup_tiles["im"] = re_ps, im_ps
            for e in range(2):
                for h in range(2):
                    nc.tensor.transpose(
                        re_ps[:, e, h * P : (h + 1) * P], unit_blocks[:, h, 0, 2 * u + e, :], ident_f32[:]
                    )
                    nc.tensor.transpose(
                        im_ps[:, e, h * P : (h + 1) * P], unit_blocks[:, h, 1, 2 * u + e, :], ident_f32[:]
                    )

        sine_products = {}

        def scale_by_sines(c):
            for name, part in (("im", setup_tiles["im"]), ("re", setup_tiles["re"])):
                scaled = setup_tmp.tile([P, B], F32, name=name + "_sin")
                nc.scalar.activation(
                    out=scaled[:], in_=part[:, c % 2, :], func=ACT.Copy, scale=sin_cos[:, 0, c : c + 1]
                )
                sine_products[(name, c)] = scaled

        def rotate_probes(c):
            cos_col = sin_cos[:, 1, c : c + 1]
            nc.vector.scalar_tensor_tensor(
                out=planes[:, 0, c, :], in0=setup_tiles["re"][:, c % 2, :], scalar=cos_col,
                in1=sine_products[("im", c)][:], op0=ALU.mult, op1=ALU.subtract,
            )
            nc.vector.scalar_tensor_tensor(
                out=planes[:, 1, c, :], in0=setup_tiles["im"][:, c % 2, :], scalar=cos_col,
                in1=sine_products[("re", c)][:], op0=ALU.mult, op1=ALU.add,
            )

        def quantise_probes():
            rot_grouped = setup.tile([P, 2, B, PACK], BF16, align_bytes=64)
            nc.vector.tensor_copy(out=rot_grouped[:], in_=planes[:].rearrange("p g k b -> p g b k"))
            nc.vector.quantize_mx(
                out=rot_codes[:].bitcast(FP8X4),
                scales=rot_scales[:],
                in_=rot_grouped[:].rearrange("p g b k -> p (g b k)"),
            )

        with tc.manual_schedule():
            nc.sync.dma_start(out=angles[:], in_=reference_angles.rearrange("(p k) -> p k", k=PACK))
            load_keys(0)
            nc.sync.dma_start(out=probes_sb[:], in_=probes.rearrange("(h p) d -> p h d", p=P))
            nc.sync.dma_start(out=u_sb[:], in_=u_weights.rearrange("(h p) f -> p h f", p=P))
            for j in range(1, KEY_BUFS):
                load_keys(j)
            nc.sync.dma_start(out=bias_rows[:], in_=k_bias.partition_broadcast(P))

            first_sin = setup.tile([P, 1], F32)
            nc.scalar.activation(out=first_sin[:], in_=zero_col[:], func=ACT.Sin)

            for step in range(N_QUADS + MX_LAG + 2):
                run(square_grouped, step - 2)
                if step == 3:
                    for c in (2, 3):
                        scale_by_sines(c)
                run(root_natural, step - 3)
                run(root_grouped, step - 3)
                run(square_natural, step)
                if step == 2:
                    for c in (0, 1):
                        scale_by_sines(c)
                if step == 0:
                    reduce_angles()
                    nc.scalar.activation(out=sin_cos[:], in_=setup_tiles["reduced"][:], func=ACT.Sin)
                    square_probes()
                for t in (HALF, HALF + 1, 1, 0):
                    run(regroup_keys, step - 1, t)
                run(square_last_keys, step - 1)
                if step < N_QUADS:
                    for pair in range(2):
                        run(add_bias_and_store, step - MX_LAG - 1, pair)
                    run(quantise_magnitudes, step - 4)
                    run(quantise_keys, step - 2)
                    run(square_trigger, step - 2)
                    run(add_grouped, step - 2, nc.gpsimd)
                    run(square_natural_rest, step)
                else:
                    run(square_trigger, step - 2)
                    run(add_grouped, step - 2, nc.vector)
                    run(quantise_magnitudes, step - 4)
                    run(quantise_keys, step - 2)
                    for pair in range(2):
                        run(add_bias_and_store, step - MX_LAG - 1, pair)
                if step == 1:
                    transpose_u()
                    quantise_u()
                    normalise_probes()
                if step == 2:
                    for c in (0, 1):
                        rotate_probes(c)
                if step == 3:
                    for c in (2, 3):
                        rotate_probes(c)
                    quantise_probes()
                for t in (HALF, HALF + 1):
                    run(transpose_keys, step, t)
                for t in range(HALF):
                    run(transpose_sums, step - 2, t)
                for t in (0, 1):
                    run(multiply, step - MX_LAG, t)
                for t in (1, 0):
                    run(transpose_keys, step, t)
                for t in (2, 3):
                    run(multiply, step - MX_LAG, t)
                if step in (1, 2):
                    transpose_probes(step - 1)
                run(load_keys, step + KEY_BUFS)
